import numpy as np
import ml_dtypes


def mxq(x, axis, fmt="e4m3"):
    dtype, down = {"e4m3": (ml_dtypes.float8_e4m3fn, 7), "e5m2": (ml_dtypes.float8_e5m2, 14)}[fmt]
    v = np.moveaxis(np.asarray(x, np.float32).astype(ml_dtypes.bfloat16).astype(np.float64), axis, -1)
    blocks = v.reshape(v.shape[:-1] + (-1, 32))
    amax = np.abs(blocks).max(-1, keepdims=True)
    byte = np.maximum(np.where(amax > 0, np.frexp(amax)[1] - 1 + 127, 0) - down, 1)
    scale = np.exp2(byte - 127.0)
    codes = (blocks / scale).astype(np.float32).astype(dtype).astype(np.float64)
    return np.moveaxis((codes * scale).reshape(v.shape), -1, axis)


WIDE = False


def mx_kscale(k):
    if not WIDE:
        return np.ones(k)
    levels = np.array([10, -10, 5, -5, 0])
    a = np.random.permutation(np.resize(levels, k // 512 * 4)).reshape(k // 512, 4)
    idx = np.arange(k)
    return np.exp2(a[idx // 512, idx % 128 // 32])


BF16 = ml_dtypes.bfloat16


def bf(x):
    return np.asarray(x, np.float32).astype(BF16)


def f64(x):
    return np.asarray(x).astype(np.float64)


B, L, D_G, D_SP, H, OUT = 8, 16, 512, 512, 8192, 128


def softmax1(m):
    e = np.exp(m - m.max())
    return e / e.sum()


def setup_inputs():
    s, u = mx_kscale(D_G), mx_kscale(D_SP)
    s2, u2 = np.concatenate([s, s])[:, None], np.concatenate([u, u])[:, None]
    mix0 = np.array([0.4, -0.4])
    return {
        "global_outputs": bf(np.random.standard_normal((B, L, D_G)) * s),
        "sp_outputs": bf(np.random.standard_normal((B, L, D_SP)) * u),
        "W_utt": bf(np.random.standard_normal((D_G + D_G, H)) * 0.5 / np.sqrt(D_G) / s2),
        "b_utt": bf(np.random.standard_normal(H) * 0.3),
        "W_sp": bf(np.random.standard_normal((D_SP + D_SP, H)) * 0.5 / np.sqrt(D_SP) / u2),
        "b_sp": bf(np.random.standard_normal(H) * 0.3),
        "W2": bf(np.random.standard_normal((H, OUT)) * 1.5 / np.sqrt(H)),
        "b2": bf(np.random.standard_normal(OUT) * 0.3),
        "mix_w": bf(mix0 + 0.1 * np.random.standard_normal(mix0.shape)),
        "gamma": bf(np.atleast_1d(1.5 + 0.1 * np.random.standard_normal())),
    }


def reference(global_outputs, sp_outputs, W_utt, b_utt, W_sp, b_sp, W2, b2, mix_w, gamma):
    gq = mxq(f64(global_outputs), 2, "e4m3")
    wu = f64(W_utt)
    g_j = gq @ mxq(wu[:D_G], 0, "e4m3")
    g_i = gq @ mxq(wu[D_G:], 0, "e4m3")
    utt_hidden = np.tanh(g_j[:, None, :, :] + g_i[:, :, None, :] + f64(b_utt))

    sq = mxq(f64(sp_outputs), 2, "e4m3")
    ws = f64(W_sp)
    s_j = sq @ mxq(ws[:D_SP], 0, "e4m3")
    s_i = sq @ mxq(ws[D_SP:], 0, "e4m3")
    sp_hidden = np.tanh(s_j[:, None, :, :] + s_i[:, :, None, :] + f64(b_sp))

    w = softmax1(f64(mix_w))
    state_hidden = f64(gamma) * (w[0] * utt_hidden + w[1] * sp_hidden)

    return np.tanh((mxq(state_hidden, 3, "e4m3") @ mxq(f64(W2), 0, "e4m3")) + f64(b2))

@@ -1,0 +1,315 @@
+from contextlib import ExitStack
+
+import concourse.masks as masks
+import concourse.mybir as mybir
+
+F32 = mybir.dt.float32
+BF16 = mybir.dt.bfloat16
+U32 = mybir.dt.uint32
+U8 = mybir.dt.uint8
+FP8X4 = mybir.dt.float8_e4m3fn_x4
+ACT = mybir.ActivationFunctionType
+ALU = mybir.AluOpType
+AXIS_X = mybir.AxisListType.X
+
+P = 128
+PACK = 4
+K_PASS = P * PACK
+B, L, D, H, OUT = 8, 16, 512, 8192, 128
+TOKENS = B * L
+PAIRS = B * L * L
+BANK = 512
+BLOCKS = PAIRS // BANK
+BATCHES = B // BLOCKS
+GROUPS = H // K_PASS
+HALVES = 2
+LAG = 2
+
+FLOPS = 4 * 2 * TOKENS * D * H + 2 * PAIRS * H * OUT
+
+
+def tile_stateencoder_pa_k_kernel(
+    tc, global_outputs, sp_outputs, W_utt, b_utt, W_sp, b_sp, W2, b2, mix_w, gamma, out
+):
+    nc = tc.nc
+    streams = ("sp", "utt")
+    tokens_dram = {"utt": global_outputs, "sp": sp_outputs}
+    weights_dram = {"utt": W_utt, "sp": W_sp}
+    bias_first_column = {"utt": 0, "sp": H // P}
+
+    with ExitStack() as ctx:
+        const = ctx.enter_context(tc.tile_pool(name="const", bufs=1))
+        stage = ctx.enter_context(tc.tile_pool(name="stage", bufs=2))
+        raw_pool = ctx.enter_context(tc.tile_pool(name="raw", bufs=4))
+        grouped_pool = ctx.enter_context(tc.tile_pool(name="grouped", bufs=2))
+        weight_pool = ctx.enter_context(tc.tile_pool(name="weights", bufs=2))
+        hidden_pool = ctx.enter_context(tc.tile_pool(name="hidden", bufs=3))
+        state_pool = ctx.enter_context(tc.tile_pool(name="state", bufs=LAG + 1))
+        result_pool = ctx.enter_context(tc.tile_pool(name="result", bufs=2))
+        acc_pool = ctx.enter_context(tc.psum_pool(name="acc", bufs=1))
+        bank_pool = ctx.enter_context(tc.psum_pool(name="bank", bufs=4))
+
+        ident_bf = const.tile([P, P], BF16, name="ident_bf")
+        masks.make_identity(nc, ident_bf[:])
+        ident_f32 = const.tile([P, P], F32, name="ident_f32")
+        masks.make_identity(nc, ident_f32[:])
+
+        def load_group(g):
+            cols = slice(g * K_PASS, (g + 1) * K_PASS)
+            raws = {}
+            for s in streams:
+                raw = raw_pool.tile([P, HALVES * PACK, K_PASS], BF16, name="raw_" + s, tag="raw")
+                nc.sync.dma_start(
+                    out=raw[:], in_=weights_dram[s][:, cols].rearrange("(v q) w -> q v w", q=P)
+                )
+                raws[s] = raw
+            raw2 = raw_pool.tile([P, PACK, OUT], BF16, name="raw2", tag="raw2")
+            nc.sync.dma_start(out=raw2[:], in_=W2[cols, :].rearrange("(t p) o -> p t o", p=P))
+            raws["W2"] = raw2
+            return raws
+
+        token_rows = {}
+        for s in streams:
+            token_rows[s] = stage.tile([P, D], BF16, name="rows_" + s, bufs=1)
+            nc.sync.dma_start(
+                out=token_rows[s][:], in_=tokens_dram[s].rearrange("b l d -> (b l) d")
+            )
+        raw_groups = {0: load_group(0), 1: load_group(1)}
+
+        token_words = {}
+        for s in streams:
+            rows = token_rows[s]
+            flipped = bank_pool.tile([P, PACK, TOKENS], BF16, name="flipped", tag="bank")
+            for u in range(PACK):
+                nc.tensor.transpose(flipped[:, u, :], rows[:, u * P : (u + 1) * P], ident_bf[:])
+            words = const.tile([P, TOKENS, PACK], BF16, name="words_" + s)
+            nc.vector.tensor_copy(out=words[:], in_=flipped[:].rearrange("p u r -> p r u"))
+            token_words[s] = words
+
+        bias_rows = const.tile([P, P], BF16, name="bias_rows")
+        nc.scalar.dma_start(out=bias_rows[0 : H // P, :], in_=b_utt.rearrange("(c p) -> c p", p=P))
+        nc.scalar.dma_start(out=bias_rows[H // P : P, :], in_=b_sp.rearrange("(c p) -> c p", p=P))
+        bias_flipped = bank_pool.tile([P, P], BF16, name="bias_flipped", tag="bank")
+        nc.tensor.transpose(bias_flipped[:], bias_rows[:], ident_bf[:])
+        bias_cols = const.tile([P, P], F32, name="bias_cols")
+        nc.vector.tensor_copy(out=bias_cols[:], in_=bias_flipped[:])
+
+        b2_rows = const.tile([P, P], BF16, name="b2_rows")
+        nc.vector.memset(b2_rows[:], 0.0)
+        nc.scalar.dma_start(out=b2_rows[0:1, :], in_=b2.rearrange("(r c) -> r c", r=1))
+        b2_flipped = bank_pool.tile([P, P], BF16, name="b2_flipped", tag="bank")
+        nc.tensor.transpose(b2_flipped[:], b2_rows[:], ident_bf[:])
+        b2_col = const.tile([P, 1], F32, name="b2_col")
+        nc.vector.tensor_copy(out=b2_col[:], in_=b2_flipped[:, 0:1])
+
+        mix_bf = const.tile([P, 2], BF16, name="mix_bf")
+        nc.scalar.dma_start(out=mix_bf[:], in_=mix_w.partition_broadcast(P))
+        gamma_bf = const.tile([P, 1], BF16, name="gamma_bf")
+        nc.scalar.dma_start(out=gamma_bf[:], in_=gamma.partition_broadcast(P))
+        mix = const.tile([P, 2], F32, name="mix")
+        nc.vector.tensor_copy(out=mix[:], in_=mix_bf[:])
+        gain = const.tile([P, 1], F32, name="gain")
+        nc.vector.tensor_copy(out=gain[:], in_=gamma_bf[:])
+        top = const.tile([P, 1], F32, name="top")
+        nc.vector.reduce_max(out=top[:], in_=mix[:], axis=AXIS_X)
+        shifted = const.tile([P, 2], F32, name="shifted")
+        nc.vector.tensor_scalar(
+            out=shifted[:], in0=mix[:], scalar1=top[:, 0:1], scalar2=None, op0=ALU.subtract
+        )
+        expd = const.tile([P, 2], F32, name="expd")
+        nc.scalar.activation(out=expd[:], in_=shifted[:], func=ACT.Exp)
+        total = const.tile([P, 1], F32, name="total")
+        nc.vector.reduce_sum(out=total[:], in_=expd[:], axis=AXIS_X)
+        inverse = const.tile([P, 1], F32, name="inverse")
+        nc.vector.reciprocal(out=inverse[:], in_=total[:])
+        coef = const.tile([P, 2], F32, name="coef")
+        nc.vector.tensor_scalar(
+            out=coef[:],
+            in0=expd[:],
+            scalar1=inverse[:, 0:1],
+            scalar2=gain[:, 0:1],
+            op0=ALU.mult,
+            op1=ALU.mult,
+        )
+
+        pair_codes = {}
+        pair_scales = {}
+        for s in streams:
+            for side in ("j", "i"):
+                pair_codes[s, side] = const.tile(
+                    [P, PAIRS], U32, name="codes_%s_%s" % (s, side), align_bytes=64
+                )
+                pair_scales[s, side] = const.tile(
+                    [P, PAIRS], U8, name="scales_%s_%s" % (s, side), align_bytes=64
+                )
+
+        def quantise_pairs(s, blk):
+            cols = slice(blk * BANK, (blk + 1) * BANK)
+            words = token_words[s][:, blk * BATCHES * L : (blk + 1) * BATCHES * L, :]
+            wide_j = stage.tile([P, BATCHES, L, L * PACK], BF16, name="wide_j", align_bytes=64)
+            nc.vector.tensor_copy(
+                out=wide_j[:],
+                in_=words.rearrange("p (b j) u -> p b (j u)", b=BATCHES)
+                .unsqueeze(2)
+                .to_broadcast([P, BATCHES, L, L * PACK]),
+            )
+            wide_i = stage.tile([P, BATCHES * L, L, PACK], BF16, name="wide_i", align_bytes=64)
+            nc.vector.tensor_copy(
+                out=wide_i[:],
+                in_=words.unsqueeze(2).to_broadcast([P, BATCHES * L, L, PACK]),
+            )
+            nc.vector.quantize_mx(
+                out=pair_codes[s, "j"][:, cols].bitcast(FP8X4),
+                scales=pair_scales[s, "j"][:, cols],
+                in_=wide_j[:].rearrange("p b i w -> p (b i w)"),
+            )
+            nc.vector.quantize_mx(
+                out=pair_codes[s, "i"][:, cols].bitcast(FP8X4),
+                scales=pair_scales[s, "i"][:, cols],
+                in_=wide_i[:].rearrange("p r j u -> p (r j u)"),
+            )
+
+        def quantise_group(raws):
+            quantised = {}
+            for s in streams:
+                grouped = grouped_pool.tile(
+                    [P, HALVES, K_PASS, PACK], BF16, name="grouped", align_bytes=64
+                )
+                for half in range(HALVES):
+                    nc.vector.tensor_copy(
+                        out=grouped[:, half].rearrange("p (c i) u -> p c u i", i=4),
+                        in_=raws[s][:, half * PACK : (half + 1) * PACK, :].rearrange(
+                            "p u (c i) -> p c u i", i=4
+                        ),
+                    )
+                codes = weight_pool.tile(
+                    [P, HALVES, K_PASS], U32, name="w_codes_" + s, align_bytes=64
+                )
+                scales = weight_pool.tile(
+                    [P, HALVES, K_PASS], U8, name="w_scales_" + s, align_bytes=64
+                )
+                nc.vector.quantize_mx(
+                    out=codes[:].rearrange("p h w -> p (h w)").bitcast(FP8X4),
+                    scales=scales[:].rearrange("p h w -> p (h w)"),
+                    in_=grouped[:].rearrange("p h w u -> p (h w u)"),
+                )
+                quantised[s] = (codes, scales)
+            grouped2 = grouped_pool.tile([P, OUT, PACK], BF16, name="grouped2", align_bytes=64)
+            nc.vector.tensor_copy(out=grouped2[:], in_=raws["W2"][:].rearrange("p t o -> p o t"))
+            codes2 = weight_pool.tile([P, OUT], U32, name="w2_codes", bufs=LAG + 2, align_bytes=64)
+            scales2 = weight_pool.tile([P, OUT], U8, name="w2_scales", bufs=LAG + 2, align_bytes=64)
+            nc.vector.quantize_mx(
+                out=codes2[:].bitcast(FP8X4),
+                scales=scales2[:],
+                in_=grouped2[:].rearrange("p o t -> p (o t)"),
+            )
+            quantised["W2"] = (codes2, scales2)
+            return quantised
+
+        for s in streams:
+            quantise_pairs(s, 0)
+        weight_groups = {0: quantise_group(raw_groups[0])}
+        for blk in range(1, BLOCKS):
+            for s in streams:
+                quantise_pairs(s, blk)
+
+        acc = [acc_pool.tile([P, BANK], F32, name="acc%d" % blk) for blk in range(BLOCKS)]
+        state_words = {}
+
+        def first_stage(g, blk):
+            cols = slice(blk * BANK, (blk + 1) * BANK)
+            hidden = {}
+            for s in streams:
+                codes, scales = weight_groups[g][s]
+                hidden[s] = hidden_pool.tile([P, PACK, BANK], F32, name="hidden_" + s)
+                for t in range(PACK):
+                    units = slice(t * P, (t + 1) * P)
+                    bank = bank_pool.tile([P, BANK], F32, name="bank", tag="bank")
+                    for half, side in enumerate(("j", "i")):
+                        nc.tensor.matmul_mx(
+                            out=bank[:],
+                            lhsT=codes[:, half, units].bitcast(FP8X4),
+                            lhsT_scale=scales[:, half, units],
+                            rhs=pair_codes[s, side][:, cols].bitcast(FP8X4),
+                            rhs_scale=pair_scales[s, side][:, cols],
+                            start=(half == 0),
+                            stop=(half == HALVES - 1),
+                        )
+                    column = bias_first_column[s] + g * PACK + t
+                    nc.scalar.activation(
+                        out=hidden[s][:, t, :],
+                        in_=bank[:],
+                        func=ACT.Tanh,
+                        bias=bias_cols[:, column : column + 1],
+                        scale=1.0,
+                    )
+            return hidden
+
+        def mix_and_quantise(hidden):
+            nc.vector.tensor_scalar(
+                out=hidden["sp"][:],
+                in0=hidden["sp"][:],
+                scalar1=coef[:, 1:2],
+                scalar2=None,
+                op0=ALU.mult,
+            )
+            state = state_pool.tile([P, BANK, PACK], BF16, name="state", bufs=2, align_bytes=64)
+            nc.vector.scalar_tensor_tensor(
+                out=state[:],
+                in0=hidden["utt"][:].rearrange("p t c -> p c t"),
+                scalar=coef[:, 0:1],
+                in1=hidden["sp"][:].rearrange("p t c -> p c t"),
+                op0=ALU.mult,
+                op1=ALU.add,
+            )
+            codes = state_pool.tile([P, BANK], U32, name="state_codes", align_bytes=64)
+            scales = state_pool.tile([P, BANK], U8, name="state_scales", align_bytes=64)
+            nc.vector.quantize_mx(
+                out=codes[:].bitcast(FP8X4),
+                scales=scales[:],
+                in_=state[:].rearrange("p c t -> p (c t)"),
+            )
+            return codes, scales
+
+        def second_stage(unit):
+            g, blk = divmod(unit, BLOCKS)
+            codes2, scales2 = weight_groups[g]["W2"]
+            codes, scales = state_words[unit]
+            nc.tensor.matmul_mx(
+                out=acc[blk][:],
+                lhsT=codes2[:].bitcast(FP8X4),
+                lhsT_scale=scales2[:],
+                rhs=codes[:].bitcast(FP8X4),
+                rhs_scale=scales[:],
+                start=(g == 0),
+                stop=(g == GROUPS - 1),
+            )
+
+        for g in range(GROUPS):
+            if g + 2 < GROUPS:
+                raw_groups[g + 2] = load_group(g + 2)
+            if g + 1 < GROUPS:
+                weight_groups[g + 1] = quantise_group(raw_groups[g + 1])
+            for blk in range(BLOCKS):
+                unit = g * BLOCKS + blk
+                state_words[unit] = mix_and_quantise(first_stage(g, blk))
+                if unit >= LAG:
+                    second_stage(unit - LAG)
+        for unit in range(GROUPS * BLOCKS - LAG, GROUPS * BLOCKS):
+            second_stage(unit)
+
+        out_rows = out.rearrange("b i j o -> (b i j) o")
+        for blk in range(BLOCKS):
+            result = result_pool.tile([P, BANK], F32, name="result")
+            nc.scalar.activation(
+                out=result[:], in_=acc[blk][:], func=ACT.Tanh, bias=b2_col[:, 0:1], scale=1.0
+            )
+            turned = bank_pool.tile([P, BANK // P, OUT], F32, name="turned", tag="bank")
+            for r in range(BANK // P):
+                nc.tensor.transpose(turned[:, r, :], result[:, r * P : (r + 1) * P], ident_f32[:])
+            rows_out = result_pool.tile([P, BANK // P, OUT], F32, name="rows_out")
+            nc.vector.tensor_copy(out=rows_out[:], in_=turned[:])
+            nc.sync.dma_start(
+                out=out_rows[blk * BANK : (blk + 1) * BANK, :].rearrange("(r p) o -> p r o", p=P),
+                in_=rows_out[:],
+            )

@@ -22,7 +22,11 @@ BANK = 512
 BLOCKS = PAIRS // BANK
 BATCHES = B // BLOCKS
 GROUPS = H // K_PASS
+UNITS = GROUPS * BLOCKS
 HALVES = 2
+STREAMS = ("sp", "utt")
+PIECES = len(STREAMS) * HALVES
+LEAD = PIECES + 1
 LAG = 2
 
 FLOPS = 4 * 2 * TOKENS * D * H + 2 * PAIRS * H * OUT
@@ -32,19 +36,19 @@ def tile_stateencoder_pa_k_kernel(
     tc, global_outputs, sp_outputs, W_utt, b_utt, W_sp, b_sp, W2, b2, mix_w, gamma, out
 ):
     nc = tc.nc
-    streams = ("sp", "utt")
     tokens_dram = {"utt": global_outputs, "sp": sp_outputs}
     weights_dram = {"utt": W_utt, "sp": W_sp}
     bias_first_column = {"utt": 0, "sp": H // P}
 
     with ExitStack() as ctx:
+        ctx.enter_context(tc.manual_schedule())
         const = ctx.enter_context(tc.tile_pool(name="const", bufs=1))
         stage = ctx.enter_context(tc.tile_pool(name="stage", bufs=2))
         raw_pool = ctx.enter_context(tc.tile_pool(name="raw", bufs=4))
-        grouped_pool = ctx.enter_context(tc.tile_pool(name="grouped", bufs=2))
+        grouped_pool = ctx.enter_context(tc.tile_pool(name="grouped", bufs=3))
         weight_pool = ctx.enter_context(tc.tile_pool(name="weights", bufs=2))
         hidden_pool = ctx.enter_context(tc.tile_pool(name="hidden", bufs=3))
-        state_pool = ctx.enter_context(tc.tile_pool(name="state", bufs=LAG + 1))
+        state_pool = ctx.enter_context(tc.tile_pool(name="state", bufs=LAG + 2))
         result_pool = ctx.enter_context(tc.tile_pool(name="result", bufs=2))
         acc_pool = ctx.enter_context(tc.psum_pool(name="acc", bufs=1))
         bank_pool = ctx.enter_context(tc.psum_pool(name="bank", bufs=4))
@@ -54,87 +58,60 @@ def tile_stateencoder_pa_k_kernel(
         ident_f32 = const.tile([P, P], F32, name="ident_f32")
         masks.make_identity(nc, ident_f32[:])
 
+        raw_groups = {}
+
         def load_group(g):
             cols = slice(g * K_PASS, (g + 1) * K_PASS)
             raws = {}
-            for s in streams:
-                raw = raw_pool.tile([P, HALVES * PACK, K_PASS], BF16, name="raw_" + s, tag="raw")
-                nc.sync.dma_start(
-                    out=raw[:], in_=weights_dram[s][:, cols].rearrange("(v q) w -> q v w", q=P)
+            raws["W2"] = raw_pool.tile([P, PACK, OUT], BF16, name="raw2", tag="raw2")
+            nc.sync.dma_start(
+                out=raws["W2"][:], in_=W2[cols, :].rearrange("(t p) o -> p t o", p=P)
+            )
+            for s in STREAMS:
+                raws[s] = raw_pool.tile(
+                    [P, HALVES * PACK, K_PASS], BF16, name="raw_" + s, tag="raw"
                 )
-                raws[s] = raw
-            raw2 = raw_pool.tile([P, PACK, OUT], BF16, name="raw2", tag="raw2")
-            nc.sync.dma_start(out=raw2[:], in_=W2[cols, :].rearrange("(t p) o -> p t o", p=P))
-            raws["W2"] = raw2
-            return raws
+                nc.sync.dma_start(
+                    out=raws[s][:],
+                    in_=weights_dram[s][:, cols].rearrange("(v q) w -> q v w", q=P),
+                )
+            raw_groups[g] = raws
 
         token_rows = {}
-        for s in streams:
+        for s in STREAMS:
             token_rows[s] = stage.tile([P, D], BF16, name="rows_" + s, bufs=1)
             nc.sync.dma_start(
                 out=token_rows[s][:], in_=tokens_dram[s].rearrange("b l d -> (b l) d")
             )
-        raw_groups = {0: load_group(0), 1: load_group(1)}
-
-        token_words = {}
-        for s in streams:
-            rows = token_rows[s]
-            flipped = bank_pool.tile([P, PACK, TOKENS], BF16, name="flipped", tag="bank")
-            for u in range(PACK):
-                nc.tensor.transpose(flipped[:, u, :], rows[:, u * P : (u + 1) * P], ident_bf[:])
-            words = const.tile([P, TOKENS, PACK], BF16, name="words_" + s)
-            nc.vector.tensor_copy(out=words[:], in_=flipped[:].rearrange("p u r -> p r u"))
-            token_words[s] = words
+        load_group(0)
+        load_group(1)
 
         bias_rows = const.tile([P, P], BF16, name="bias_rows")
         nc.scalar.dma_start(out=bias_rows[0 : H // P, :], in_=b_utt.rearrange("(c p) -> c p", p=P))
         nc.scalar.dma_start(out=bias_rows[H // P : P, :], in_=b_sp.rearrange("(c p) -> c p", p=P))
-        bias_flipped = bank_pool.tile([P, P], BF16, name="bias_flipped", tag="bank")
-        nc.tensor.transpose(bias_flipped[:], bias_rows[:], ident_bf[:])
-        bias_cols = const.tile([P, P], F32, name="bias_cols")
-        nc.vector.tensor_copy(out=bias_cols[:], in_=bias_flipped[:])
-
-        b2_rows = const.tile([P, P], BF16, name="b2_rows")
-        nc.vector.memset(b2_rows[:], 0.0)
-        nc.scalar.dma_start(out=b2_rows[0:1, :], in_=b2.rearrange("(r c) -> r c", r=1))
-        b2_flipped = bank_pool.tile([P, P], BF16, name="b2_flipped", tag="bank")
-        nc.tensor.transpose(b2_flipped[:], b2_rows[:], ident_bf[:])
-        b2_col = const.tile([P, 1], F32, name="b2_col")
-        nc.vector.tensor_copy(out=b2_col[:], in_=b2_flipped[:, 0:1])
-
         mix_bf = const.tile([P, 2], BF16, name="mix_bf")
         nc.scalar.dma_start(out=mix_bf[:], in_=mix_w.partition_broadcast(P))
         gamma_bf = const.tile([P, 1], BF16, name="gamma_bf")
         nc.scalar.dma_start(out=gamma_bf[:], in_=gamma.partition_broadcast(P))
-        mix = const.tile([P, 2], F32, name="mix")
-        nc.vector.tensor_copy(out=mix[:], in_=mix_bf[:])
-        gain = const.tile([P, 1], F32, name="gain")
-        nc.vector.tensor_copy(out=gain[:], in_=gamma_bf[:])
-        top = const.tile([P, 1], F32, name="top")
-        nc.vector.reduce_max(out=top[:], in_=mix[:], axis=AXIS_X)
-        shifted = const.tile([P, 2], F32, name="shifted")
-        nc.vector.tensor_scalar(
-            out=shifted[:], in0=mix[:], scalar1=top[:, 0:1], scalar2=None, op0=ALU.subtract
-        )
-        expd = const.tile([P, 2], F32, name="expd")
-        nc.scalar.activation(out=expd[:], in_=shifted[:], func=ACT.Exp)
-        total = const.tile([P, 1], F32, name="total")
-        nc.vector.reduce_sum(out=total[:], in_=expd[:], axis=AXIS_X)
-        inverse = const.tile([P, 1], F32, name="inverse")
-        nc.vector.reciprocal(out=inverse[:], in_=total[:])
-        coef = const.tile([P, 2], F32, name="coef")
-        nc.vector.tensor_scalar(
-            out=coef[:],
-            in0=expd[:],
-            scalar1=inverse[:, 0:1],
-            scalar2=gain[:, 0:1],
-            op0=ALU.mult,
-            op1=ALU.mult,
-        )
+        b2_rows = const.tile([P, P], BF16, name="b2_rows")
+        nc.vector.memset(b2_rows[:], 0.0)
+        nc.scalar.dma_start(out=b2_rows[0:1, :], in_=b2.rearrange("(r c) -> r c", r=1))
+
+        token_words = {}
+        for s in STREAMS:
+            flipped = bank_pool.tile([P, PACK, TOKENS], BF16, name="flipped", tag="bank")
+            for u in range(PACK):
+                nc.tensor.transpose(
+                    flipped[:, u, :], token_rows[s][:, u * P : (u + 1) * P], ident_bf[:]
+                )
+            token_words[s] = const.tile([P, TOKENS, PACK], BF16, name="words_" + s)
+            nc.vector.tensor_copy(
+                out=token_words[s][:], in_=flipped[:].rearrange("p u r -> p r u")
+            )
 
         pair_codes = {}
         pair_scales = {}
-        for s in streams:
+        for s in STREAMS:
             for side in ("j", "i"):
                 pair_codes[s, side] = const.tile(
                     [P, PAIRS], U32, name="codes_%s_%s" % (s, side), align_bytes=64
@@ -169,59 +146,106 @@ def tile_stateencoder_pa_k_kernel(
                 in_=wide_i[:].rearrange("p r j u -> p (r j u)"),
             )
 
-        def quantise_group(raws):
-            quantised = {}
-            for s in streams:
-                grouped = grouped_pool.tile(
-                    [P, HALVES, K_PASS, PACK], BF16, name="grouped", align_bytes=64
-                )
-                for half in range(HALVES):
-                    nc.vector.tensor_copy(
-                        out=grouped[:, half].rearrange("p (c i) u -> p c u i", i=4),
-                        in_=raws[s][:, half * PACK : (half + 1) * PACK, :].rearrange(
-                            "p u (c i) -> p c u i", i=4
-                        ),
-                    )
-                codes = weight_pool.tile(
-                    [P, HALVES, K_PASS], U32, name="w_codes_" + s, align_bytes=64
-                )
-                scales = weight_pool.tile(
-                    [P, HALVES, K_PASS], U8, name="w_scales_" + s, align_bytes=64
-                )
-                nc.vector.quantize_mx(
-                    out=codes[:].rearrange("p h w -> p (h w)").bitcast(FP8X4),
-                    scales=scales[:].rearrange("p h w -> p (h w)"),
-                    in_=grouped[:].rearrange("p h w u -> p (h w u)"),
-                )
-                quantised[s] = (codes, scales)
-            grouped2 = grouped_pool.tile([P, OUT, PACK], BF16, name="grouped2", align_bytes=64)
-            nc.vector.tensor_copy(out=grouped2[:], in_=raws["W2"][:].rearrange("p t o -> p o t"))
-            codes2 = weight_pool.tile([P, OUT], U32, name="w2_codes", bufs=LAG + 2, align_bytes=64)
-            scales2 = weight_pool.tile([P, OUT], U8, name="w2_scales", bufs=LAG + 2, align_bytes=64)
-            nc.vector.quantize_mx(
-                out=codes2[:].bitcast(FP8X4),
-                scales=scales2[:],
-                in_=grouped2[:].rearrange("p o t -> p (o t)"),
-            )
-            quantised["W2"] = (codes2, scales2)
-            return quantised
-
-        for s in streams:
+        for s in STREAMS:
             quantise_pairs(s, 0)
-        weight_groups = {0: quantise_group(raw_groups[0])}
-        for blk in range(1, BLOCKS):
-            for s in streams:
-                quantise_pairs(s, blk)
+
+        bias_flipped = bank_pool.tile([P, P], BF16, name="bias_flipped", tag="bank")
+        nc.tensor.transpose(bias_flipped[:], bias_rows[:], ident_bf[:])
+        bias_cols = const.tile([P, P], F32, name="bias_cols")
+        nc.vector.tensor_copy(out=bias_cols[:], in_=bias_flipped[:])
+        b2_flipped = bank_pool.tile([P, P], BF16, name="b2_flipped", tag="bank")
+        nc.tensor.transpose(b2_flipped[:], b2_rows[:], ident_bf[:])
+        b2_col = const.tile([P, 1], F32, name="b2_col")
+        nc.vector.tensor_copy(out=b2_col[:], in_=b2_flipped[:, 0:1])
+
+        mix = const.tile([P, 2], F32, name="mix")
+        nc.vector.tensor_copy(out=mix[:], in_=mix_bf[:])
+        gain = const.tile([P, 1], F32, name="gain")
+        nc.vector.tensor_copy(out=gain[:], in_=gamma_bf[:])
+        top = const.tile([P, 1], F32, name="top")
+        nc.vector.reduce_max(out=top[:], in_=mix[:], axis=AXIS_X)
+        shifted = const.tile([P, 2], F32, name="shifted")
+        nc.vector.tensor_scalar(
+            out=shifted[:], in0=mix[:], scalar1=top[:, 0:1], scalar2=None, op0=ALU.subtract
+        )
+        expd = const.tile([P, 2], F32, name="expd")
+        nc.scalar.activation(out=expd[:], in_=shifted[:], func=ACT.Exp)
+        total = const.tile([P, 1], F32, name="total")
+        nc.vector.reduce_sum(out=total[:], in_=expd[:], axis=AXIS_X)
+        inverse = const.tile([P, 1], F32, name="inverse")
+        nc.vector.reciprocal(out=inverse[:], in_=total[:])
+        coef = const.tile([P, 2], F32, name="coef")
+        nc.vector.tensor_scalar(
+            out=coef[:],
+            in0=expd[:],
+            scalar1=inverse[:, 0:1],
+            scalar2=gain[:, 0:1],
+            op0=ALU.mult,
+            op1=ALU.mult,
+        )
+
+        grouped_pieces = {}
+        weight_words = {}
+
+        def regroup_piece(m):
+            g, piece = divmod(m, PIECES)
+            s, half = STREAMS[piece // HALVES], piece % HALVES
+            grouped = grouped_pool.tile([P, K_PASS, PACK], BF16, name="grouped", align_bytes=64)
+            nc.vector.tensor_copy(
+                out=grouped[:].rearrange("p (c i) u -> p c u i", i=4),
+                in_=raw_groups[g][s][:, half * PACK : (half + 1) * PACK, :].rearrange(
+                    "p u (c i) -> p c u i", i=4
+                ),
+            )
+            grouped_pieces[m] = grouped
+            if piece == 0:
+                grouped2 = grouped_pool.tile([P, OUT, PACK], BF16, name="grouped2", align_bytes=64)
+                nc.scalar.copy(out=grouped2[:], in_=raw_groups[g]["W2"][:].rearrange("p t o -> p o t"))
+                grouped_pieces["W2", g] = grouped2
+            if piece == PIECES - 1 and g + 2 < GROUPS:
+                load_group(g + 2)
+
+        def quantise_piece(m):
+            g, piece = divmod(m, PIECES)
+            s, half = STREAMS[piece // HALVES], piece % HALVES
+            if half == 0:
+                weight_words[g, s] = (
+                    weight_pool.tile([P, HALVES, K_PASS], U32, name="w_codes_" + s, align_bytes=64),
+                    weight_pool.tile([P, HALVES, K_PASS], U8, name="w_scales_" + s, align_bytes=64),
+                )
+            codes, scales = weight_words[g, s]
+            nc.vector.quantize_mx(
+                out=codes[:, half, :].bitcast(FP8X4),
+                scales=scales[:, half, :],
+                in_=grouped_pieces[m][:].rearrange("p w u -> p (w u)"),
+            )
+            if piece == 0:
+                codes2 = weight_pool.tile([P, OUT], U32, name="w2_codes", bufs=4, align_bytes=64)
+                scales2 = weight_pool.tile([P, OUT], U8, name="w2_scales", bufs=4, align_bytes=64)
+                nc.vector.quantize_mx(
+                    out=codes2[:].bitcast(FP8X4),
+                    scales=scales2[:],
+                    in_=grouped_pieces["W2", g][:].rearrange("p o t -> p (o t)"),
+                )
+                weight_words[g, "W2"] = (codes2, scales2)
+
+        def prepare_weights(unit):
+            if unit + LEAD + 1 < GROUPS * PIECES:
+                regroup_piece(unit + LEAD + 1)
+            if 0 <= unit + LEAD < GROUPS * PIECES:
+                quantise_piece(unit + LEAD)
 
         acc = [acc_pool.tile([P, BANK], F32, name="acc%d" % blk) for blk in range(BLOCKS)]
+        hidden_tiles = {}
+        state_tiles = {}
         state_words = {}
 
-        def first_stage(g, blk):
+        def first_stage(unit):
+            g, blk = divmod(unit, BLOCKS)
             cols = slice(blk * BANK, (blk + 1) * BANK)
-            hidden = {}
-            for s in streams:
-                codes, scales = weight_groups[g][s]
-                hidden[s] = hidden_pool.tile([P, PACK, BANK], F32, name="hidden_" + s)
+            for s in STREAMS:
+                codes, scales = weight_words[g, s]
+                hidden = hidden_pool.tile([P, PACK, BANK], F32, name="hidden_" + s)
                 for t in range(PACK):
                     units = slice(t * P, (t + 1) * P)
                     bank = bank_pool.tile([P, BANK], F32, name="bank", tag="bank")
@@ -237,69 +261,45 @@ def tile_stateencoder_pa_k_kernel(
                         )
                     column = bias_first_column[s] + g * PACK + t
                     nc.scalar.activation(
-                        out=hidden[s][:, t, :],
+                        out=hidden[:, t, :],
                         in_=bank[:],
                         func=ACT.Tanh,
                         bias=bias_cols[:, column : column + 1],
                         scale=1.0,
                     )
-            return hidden
+                hidden_tiles[unit, s] = hidden
 
-        def mix_and_quantise(hidden):
+        def scale_sp(unit):
+            hidden_sp = hidden_tiles[unit, "sp"]
             nc.vector.tensor_scalar(
-                out=hidden["sp"][:],
-                in0=hidden["sp"][:],
-                scalar1=coef[:, 1:2],
-                scalar2=None,
-                op0=ALU.mult,
+                out=hidden_sp[:], in0=hidden_sp[:], scalar1=coef[:, 1:2], scalar2=None, op0=ALU.mult
             )
+
+        def mix_streams(unit):
             state = state_pool.tile([P, BANK, PACK], BF16, name="state", bufs=2, align_bytes=64)
             nc.vector.scalar_tensor_tensor(
                 out=state[:],
-                in0=hidden["utt"][:].rearrange("p t c -> p c t"),
+                in0=hidden_tiles[unit, "utt"][:].rearrange("p t c -> p c t"),
                 scalar=coef[:, 0:1],
-                in1=hidden["sp"][:].rearrange("p t c -> p c t"),
+                in1=hidden_tiles[unit, "sp"][:].rearrange("p t c -> p c t"),
                 op0=ALU.mult,
                 op1=ALU.add,
             )
+            state_tiles[unit] = state
+
+        def quantise_state(unit):
             codes = state_pool.tile([P, BANK], U32, name="state_codes", align_bytes=64)
             scales = state_pool.tile([P, BANK], U8, name="state_scales", align_bytes=64)
             nc.vector.quantize_mx(
                 out=codes[:].bitcast(FP8X4),
                 scales=scales[:],
-                in_=state[:].rearrange("p c t -> p (c t)"),
+                in_=state_tiles[unit][:].rearrange("p c t -> p (c t)"),
             )
-            return codes, scales
-
-        def second_stage(unit):
-            g, blk = divmod(unit, BLOCKS)
-            codes2, scales2 = weight_groups[g]["W2"]
-            codes, scales = state_words[unit]
-            nc.tensor.matmul_mx(
-                out=acc[blk][:],
-                lhsT=codes2[:].bitcast(FP8X4),
-                lhsT_scale=scales2[:],
-                rhs=codes[:].bitcast(FP8X4),
-                rhs_scale=scales[:],
-                start=(g == 0),
-                stop=(g == GROUPS - 1),
-            )
-
-        for g in range(GROUPS):
-            if g + 2 < GROUPS:
-                raw_groups[g + 2] = load_group(g + 2)
-            if g + 1 < GROUPS:
-                weight_groups[g + 1] = quantise_group(raw_groups[g + 1])
-            for blk in range(BLOCKS):
-                unit = g * BLOCKS + blk
-                state_words[unit] = mix_and_quantise(first_stage(g, blk))
-                if unit >= LAG:
-                    second_stage(unit - LAG)
-        for unit in range(GROUPS * BLOCKS - LAG, GROUPS * BLOCKS):
-            second_stage(unit)
+            state_words[unit] = (codes, scales)
 
         out_rows = out.rearrange("b i j o -> (b i j) o")
-        for blk in range(BLOCKS):
+
+        def finish_block(blk):
             result = result_pool.tile([P, BANK], F32, name="result")
             nc.scalar.activation(
                 out=result[:], in_=acc[blk][:], func=ACT.Tanh, bias=b2_col[:, 0:1], scale=1.0
@@ -313,3 +313,37 @@ def tile_stateencoder_pa_k_kernel(
                 out=out_rows[blk * BANK : (blk + 1) * BANK, :].rearrange("(r p) o -> p r o", p=P),
                 in_=rows_out[:],
             )
+
+        def second_stage(unit):
+            g, blk = divmod(unit, BLOCKS)
+            codes2, scales2 = weight_words[g, "W2"]
+            codes, scales = state_words[unit]
+            nc.tensor.matmul_mx(
+                out=acc[blk][:],
+                lhsT=codes2[:].bitcast(FP8X4),
+                lhsT_scale=scales2[:],
+                rhs=codes[:].bitcast(FP8X4),
+                rhs_scale=scales[:],
+                start=(g == 0),
+                stop=(g == GROUPS - 1),
+            )
+            if g == GROUPS - 1:
+                finish_block(blk)
+
+        for unit in range(-(LEAD + 1), 0):
+            prepare_weights(unit)
+        for blk in range(1, BLOCKS):
+            for s in STREAMS:
+                quantise_pairs(s, blk)
+
+        for unit in range(UNITS + LAG):
+            if unit < UNITS:
+                first_stage(unit)
+                scale_sp(unit)
+            if 1 <= unit <= UNITS:
+                quantise_state(unit - 1)
+            if unit < UNITS:
+                mix_streams(unit)
+                prepare_weights(unit)
+            if unit >= LAG:
+                second_stage(unit - LAG)

@@ -10,7 +10,6 @@ U8 = mybir.dt.uint8
 FP8X4 = mybir.dt.float8_e4m3fn_x4
 ACT = mybir.ActivationFunctionType
 ALU = mybir.AluOpType
-AXIS_X = mybir.AxisListType.X
 
 P = 128
 PACK = 4
@@ -28,6 +27,7 @@ STREAMS = ("sp", "utt")
 PIECES = len(STREAMS) * HALVES
 LEAD = PIECES + 1
 LAG = 2
+MAX_LOGIT_GAP = 40.0
 
 FLOPS = 4 * 2 * TOKENS * D * H + 2 * PAIRS * H * OUT
 
@@ -162,27 +162,23 @@ def tile_stateencoder_pa_k_kernel(
         nc.vector.tensor_copy(out=mix[:], in_=mix_bf[:])
         gain = const.tile([P, 1], F32, name="gain")
         nc.vector.tensor_copy(out=gain[:], in_=gamma_bf[:])
-        top = const.tile([P, 1], F32, name="top")
-        nc.vector.reduce_max(out=top[:], in_=mix[:], axis=AXIS_X)
-        shifted = const.tile([P, 2], F32, name="shifted")
+        gap = const.tile([P, 1], F32, name="gap")
         nc.vector.tensor_scalar(
-            out=shifted[:], in0=mix[:], scalar1=top[:, 0:1], scalar2=None, op0=ALU.subtract
+            out=gap[:],
+            in0=mix[:, 0:1],
+            scalar1=mix[:, 1:2],
+            scalar2=MAX_LOGIT_GAP,
+            op0=ALU.subtract,
+            op1=ALU.min,
         )
-        expd = const.tile([P, 2], F32, name="expd")
-        nc.scalar.activation(out=expd[:], in_=shifted[:], func=ACT.Exp)
-        total = const.tile([P, 1], F32, name="total")
-        nc.vector.reduce_sum(out=total[:], in_=expd[:], axis=AXIS_X)
-        inverse = const.tile([P, 1], F32, name="inverse")
-        nc.vector.reciprocal(out=inverse[:], in_=total[:])
-        coef = const.tile([P, 2], F32, name="coef")
-        nc.vector.tensor_scalar(
-            out=coef[:],
-            in0=expd[:],
-            scalar1=inverse[:, 0:1],
-            scalar2=gain[:, 0:1],
-            op0=ALU.mult,
-            op1=ALU.mult,
-        )
+        ratio = const.tile([P, 1], F32, name="ratio")
+        nc.scalar.activation(out=ratio[:], in_=gap[:], func=ACT.Exp)
+        denominator = const.tile([P, 1], F32, name="denominator")
+        nc.vector.tensor_scalar_add(out=denominator[:], in0=ratio[:], scalar1=1.0)
+        weight_sp = const.tile([P, 1], F32, name="weight_sp")
+        nc.vector.reciprocal(out=weight_sp[:], in_=denominator[:])
+        gain_sp = const.tile([P, 1], F32, name="gain_sp")
+        nc.vector.tensor_mul(out=gain_sp[:], in0=weight_sp[:], in1=gain[:])
 
         grouped_pieces = {}
         weight_words = {}
@@ -229,9 +225,11 @@ def tile_stateencoder_pa_k_kernel(
                 )
                 weight_words[g, "W2"] = (codes2, scales2)
 
-        def prepare_weights(unit):
+        def regroup_beside(unit):
             if unit + LEAD + 1 < GROUPS * PIECES:
                 regroup_piece(unit + LEAD + 1)
+
+        def quantise_beside(unit):
             if 0 <= unit + LEAD < GROUPS * PIECES:
                 quantise_piece(unit + LEAD)
 
@@ -269,21 +267,25 @@ def tile_stateencoder_pa_k_kernel(
                     )
                 hidden_tiles[unit, s] = hidden
 
-        def scale_sp(unit):
-            hidden_sp = hidden_tiles[unit, "sp"]
-            nc.vector.tensor_scalar(
-                out=hidden_sp[:], in0=hidden_sp[:], scalar1=coef[:, 1:2], scalar2=None, op0=ALU.mult
-            )
-
         def mix_streams(unit):
-            state = state_pool.tile([P, BANK, PACK], BF16, name="state", bufs=2, align_bytes=64)
+            hidden_utt = hidden_tiles[unit, "utt"]
             nc.vector.scalar_tensor_tensor(
-                out=state[:],
-                in0=hidden_tiles[unit, "utt"][:].rearrange("p t c -> p c t"),
-                scalar=coef[:, 0:1],
-                in1=hidden_tiles[unit, "sp"][:].rearrange("p t c -> p c t"),
+                out=hidden_utt[:],
+                in0=hidden_utt[:],
+                scalar=ratio[:, 0:1],
+                in1=hidden_tiles[unit, "sp"][:],
                 op0=ALU.mult,
                 op1=ALU.add,
+            )
+
+        def round_state(unit):
+            state = state_pool.tile([P, BANK, PACK], BF16, name="state", bufs=2, align_bytes=64)
+            nc.vector.tensor_scalar(
+                out=state[:].rearrange("p (c i) t -> p c t i", i=4),
+                in0=hidden_tiles[unit, "utt"][:].rearrange("p t (c i) -> p c t i", i=4),
+                scalar1=gain_sp[:, 0:1],
+                scalar2=None,
+                op0=ALU.mult,
             )
             state_tiles[unit] = state
 
@@ -331,7 +333,8 @@ def tile_stateencoder_pa_k_kernel(
                 finish_block(blk)
 
         for unit in range(-(LEAD + 1), 0):
-            prepare_weights(unit)
+            regroup_beside(unit)
+            quantise_beside(unit)
         for blk in range(1, BLOCKS):
             for s in STREAMS:
                 quantise_pairs(s, blk)
@@ -339,11 +342,10 @@ def tile_stateencoder_pa_k_kernel(
         for unit in range(UNITS + LAG):
             if unit < UNITS:
                 first_stage(unit)
-                scale_sp(unit)
-            if 1 <= unit <= UNITS:
-                quantise_state(unit - 1)
-            if unit < UNITS:
                 mix_streams(unit)
-                prepare_weights(unit)
+                regroup_beside(unit)
+                round_state(unit)
+                quantise_beside(unit)
+                quantise_state(unit)
             if unit >= LAG:
                 second_stage(unit - LAG)

@@ -7,6 +7,7 @@ F32 = mybir.dt.float32
 BF16 = mybir.dt.bfloat16
 U32 = mybir.dt.uint32
 U8 = mybir.dt.uint8
+I32 = mybir.dt.int32
 FP8X4 = mybir.dt.float8_e4m3fn_x4
 ACT = mybir.ActivationFunctionType
 ALU = mybir.AluOpType
@@ -14,12 +15,12 @@ ALU = mybir.AluOpType
 P = 128
 PACK = 4
 K_PASS = P * PACK
+WORD = 4
 B, L, D, H, OUT = 8, 16, 512, 8192, 128
 TOKENS = B * L
 PAIRS = B * L * L
 BANK = 512
 BLOCKS = PAIRS // BANK
-BATCHES = B // BLOCKS
 GROUPS = H // K_PASS
 UNITS = GROUPS * BLOCKS
 HALVES = 2
@@ -27,6 +28,7 @@ STREAMS = ("sp", "utt")
 PIECES = len(STREAMS) * HALVES
 LEAD = PIECES + 1
 LAG = 2
+SCALAR_COLUMNS = 128
 MAX_LOGIT_GAP = 40.0
 
 FLOPS = 4 * 2 * TOKENS * D * H + 2 * PAIRS * H * OUT
@@ -111,7 +113,9 @@ def tile_stateencoder_pa_k_kernel(
 
         pair_codes = {}
         pair_scales = {}
-        for s in STREAMS:
+
+        def quantise_tokens(s):
+            words = token_words[s]
             for side in ("j", "i"):
                 pair_codes[s, side] = const.tile(
                     [P, PAIRS], U32, name="codes_%s_%s" % (s, side), align_bytes=64
@@ -119,35 +123,53 @@ def tile_stateencoder_pa_k_kernel(
                 pair_scales[s, side] = const.tile(
                     [P, PAIRS], U8, name="scales_%s_%s" % (s, side), align_bytes=64
                 )
-
-        def quantise_pairs(s, blk):
-            cols = slice(blk * BANK, (blk + 1) * BANK)
-            words = token_words[s][:, blk * BATCHES * L : (blk + 1) * BATCHES * L, :]
-            wide_j = stage.tile([P, BATCHES, L, L * PACK], BF16, name="wide_j", align_bytes=64)
+            codes = const.tile([P, TOKENS], U32, name="codes_" + s, align_bytes=64)
+            scales = const.tile([P, TOKENS], U8, name="scales_" + s, align_bytes=64)
+            fourfold = stage.tile([P, TOKENS, WORD, PACK], BF16, name="fourfold", align_bytes=64)
+            codes_fourfold = stage.tile([P, TOKENS * WORD], U32, name="codes_fourfold", align_bytes=64)
+            scales_fourfold = const.tile([P, TOKENS * WORD], U8, name="scales4_" + s, align_bytes=64)
+            nc.vector.memset(scales[:].bitcast(I32), 0)
+            nc.vector.memset(scales_fourfold[:].bitcast(I32), 0)
             nc.vector.tensor_copy(
-                out=wide_j[:],
-                in_=words.rearrange("p (b j) u -> p b (j u)", b=BATCHES)
+                out=fourfold[:], in_=words[:].unsqueeze(2).to_broadcast([P, TOKENS, WORD, PACK])
+            )
+            nc.vector.quantize_mx(
+                out=codes[:].bitcast(FP8X4),
+                scales=scales[:],
+                in_=words[:].rearrange("p r u -> p (r u)"),
+            )
+            nc.vector.quantize_mx(
+                out=codes_fourfold[:].bitcast(FP8X4),
+                scales=scales_fourfold[:],
+                in_=fourfold[:].rearrange("p r f u -> p (r f u)"),
+            )
+            nc.vector.tensor_copy(
+                out=pair_codes[s, "j"][:].bitcast(I32).rearrange("p (b i j) -> p b i j", b=B, i=L),
+                in_=codes[:]
+                .bitcast(I32)
+                .rearrange("p (b j) -> p b j", b=B)
                 .unsqueeze(2)
-                .to_broadcast([P, BATCHES, L, L * PACK]),
+                .to_broadcast([P, B, L, L]),
             )
-            wide_i = stage.tile([P, BATCHES * L, L, PACK], BF16, name="wide_i", align_bytes=64)
             nc.vector.tensor_copy(
-                out=wide_i[:],
-                in_=words.unsqueeze(2).to_broadcast([P, BATCHES * L, L, PACK]),
+                out=pair_scales[s, "j"][:].bitcast(I32).rearrange("p (b i w) -> p b i w", b=B, i=L),
+                in_=scales[:]
+                .bitcast(I32)
+                .rearrange("p (b w) -> p b w", b=B)
+                .unsqueeze(2)
+                .to_broadcast([P, B, L, L // WORD]),
             )
-            nc.vector.quantize_mx(
-                out=pair_codes[s, "j"][:, cols].bitcast(FP8X4),
-                scales=pair_scales[s, "j"][:, cols],
-                in_=wide_j[:].rearrange("p b i w -> p (b i w)"),
+            nc.vector.tensor_copy(
+                out=pair_codes[s, "i"][:].bitcast(I32).rearrange("p (r j) -> p r j", j=L),
+                in_=codes[:].bitcast(I32).unsqueeze(2).to_broadcast([P, TOKENS, L]),
             )
-            nc.vector.quantize_mx(
-                out=pair_codes[s, "i"][:, cols].bitcast(FP8X4),
-                scales=pair_scales[s, "i"][:, cols],
-                in_=wide_i[:].rearrange("p r j u -> p (r j u)"),
+            nc.vector.tensor_copy(
+                out=pair_scales[s, "i"][:].bitcast(I32).rearrange("p (r w) -> p r w", w=L // WORD),
+                in_=scales_fourfold[:].bitcast(I32).unsqueeze(2).to_broadcast([P, TOKENS, L // WORD]),
             )
 
         for s in STREAMS:
-            quantise_pairs(s, 0)
+            quantise_tokens(s)
 
         bias_flipped = bank_pool.tile([P, P], BF16, name="bias_flipped", tag="bank")
         nc.tensor.transpose(bias_flipped[:], bias_rows[:], ident_bf[:])
@@ -187,12 +209,16 @@ def tile_stateencoder_pa_k_kernel(
             g, piece = divmod(m, PIECES)
             s, half = STREAMS[piece // HALVES], piece % HALVES
             grouped = grouped_pool.tile([P, K_PASS, PACK], BF16, name="grouped", align_bytes=64)
-            nc.vector.tensor_copy(
-                out=grouped[:].rearrange("p (c i) u -> p c u i", i=4),
-                in_=raw_groups[g][s][:, half * PACK : (half + 1) * PACK, :].rearrange(
-                    "p u (c i) -> p c u i", i=4
-                ),
-            )
+            rows = slice(half * PACK, (half + 1) * PACK)
+            split = K_PASS - SCALAR_COLUMNS
+            for copy, cols in (
+                (nc.vector.tensor_copy, slice(0, split)),
+                (nc.scalar.copy, slice(split, K_PASS)),
+            ):
+                copy(
+                    out=grouped[:, cols, :].rearrange("p (c i) u -> p c u i", i=4),
+                    in_=raw_groups[g][s][:, rows, cols].rearrange("p u (c i) -> p c u i", i=4),
+                )
             grouped_pieces[m] = grouped
             if piece == 0:
                 grouped2 = grouped_pool.tile([P, OUT, PACK], BF16, name="grouped2", align_bytes=64)
@@ -335,10 +361,6 @@ def tile_stateencoder_pa_k_kernel(
         for unit in range(-(LEAD + 1), 0):
             regroup_beside(unit)
             quantise_beside(unit)
-        for blk in range(1, BLOCKS):
-            for s in STREAMS:
-                quantise_pairs(s, blk)
-
         for unit in range(UNITS + LAG):
             if unit < UNITS:
                 first_stage(unit)

@@ -16,6 +16,7 @@ P = 128
 PACK = 4
 K_PASS = P * PACK
 WORD = 4
+RUN = 4
 B, L, D, H, OUT = 8, 16, 512, 8192, 128
 TOKENS = B * L
 PAIRS = B * L * L
@@ -23,11 +24,13 @@ BANK = 512
 BLOCKS = PAIRS // BANK
 GROUPS = H // K_PASS
 UNITS = GROUPS * BLOCKS
-HALVES = 2
 STREAMS = ("sp", "utt")
+SIDES = ("j", "i")
+HALVES = len(SIDES)
 PIECES = len(STREAMS) * HALVES
-LEAD = PIECES + 1
+ALL_PIECES = GROUPS * PIECES
 LAG = 2
+LEAD = PIECES + LAG
 SCALAR_COLUMNS = 128
 MAX_LOGIT_GAP = 40.0
 
@@ -48,8 +51,8 @@ def tile_stateencoder_pa_k_kernel(
         stage = ctx.enter_context(tc.tile_pool(name="stage", bufs=2))
         raw_pool = ctx.enter_context(tc.tile_pool(name="raw", bufs=4))
         grouped_pool = ctx.enter_context(tc.tile_pool(name="grouped", bufs=3))
-        weight_pool = ctx.enter_context(tc.tile_pool(name="weights", bufs=2))
-        hidden_pool = ctx.enter_context(tc.tile_pool(name="hidden", bufs=3))
+        weight_pool = ctx.enter_context(tc.tile_pool(name="weights", bufs=3))
+        hidden_pool = ctx.enter_context(tc.tile_pool(name="hidden", bufs=LAG + 1))
         state_pool = ctx.enter_context(tc.tile_pool(name="state", bufs=LAG + 2))
         result_pool = ctx.enter_context(tc.tile_pool(name="result", bufs=2))
         acc_pool = ctx.enter_context(tc.psum_pool(name="acc", bufs=1))
@@ -63,25 +66,25 @@ def tile_stateencoder_pa_k_kernel(
         raw_groups = {}
 
         def load_group(g):
-            cols = slice(g * K_PASS, (g + 1) * K_PASS)
+            hidden_range = slice(g * K_PASS, (g + 1) * K_PASS)
             raws = {}
-            raws["W2"] = raw_pool.tile([P, PACK, OUT], BF16, name="raw2", tag="raw2")
+            raws["W2"] = raw_pool.tile([P, PACK, OUT], BF16, name="raw_w2")
             nc.sync.dma_start(
-                out=raws["W2"][:], in_=W2[cols, :].rearrange("(t p) o -> p t o", p=P)
+                out=raws["W2"][:], in_=W2[hidden_range, :].rearrange("(t p) o -> p t o", p=P)
             )
             for s in STREAMS:
                 raws[s] = raw_pool.tile(
-                    [P, HALVES * PACK, K_PASS], BF16, name="raw_" + s, tag="raw"
+                    [P, HALVES * PACK, K_PASS], BF16, name="raw_" + s, tag="raw_w"
                 )
                 nc.sync.dma_start(
                     out=raws[s][:],
-                    in_=weights_dram[s][:, cols].rearrange("(v q) w -> q v w", q=P),
+                    in_=weights_dram[s][:, hidden_range].rearrange("(v q) w -> q v w", q=P),
                 )
             raw_groups[g] = raws
 
         token_rows = {}
         for s in STREAMS:
-            token_rows[s] = stage.tile([P, D], BF16, name="rows_" + s, bufs=1)
+            token_rows[s] = const.tile([P, D], BF16, name="token_rows_" + s)
             nc.sync.dma_start(
                 out=token_rows[s][:], in_=tokens_dram[s].rearrange("b l d -> (b l) d")
             )
@@ -99,53 +102,66 @@ def tile_stateencoder_pa_k_kernel(
         nc.vector.memset(b2_rows[:], 0.0)
         nc.scalar.dma_start(out=b2_rows[0:1, :], in_=b2.rearrange("(r c) -> r c", r=1))
 
-        token_words = {}
+        token_grouped = {}
         for s in STREAMS:
             flipped = bank_pool.tile([P, PACK, TOKENS], BF16, name="flipped", tag="bank")
             for u in range(PACK):
                 nc.tensor.transpose(
                     flipped[:, u, :], token_rows[s][:, u * P : (u + 1) * P], ident_bf[:]
                 )
-            token_words[s] = const.tile([P, TOKENS, PACK], BF16, name="words_" + s)
-            nc.vector.tensor_copy(
-                out=token_words[s][:], in_=flipped[:].rearrange("p u r -> p r u")
+            token_grouped[s] = const.tile(
+                [P, TOKENS, PACK], BF16, name="token_grouped_" + s, align_bytes=64
             )
+            nc.scalar.copy(out=token_grouped[s][:], in_=flipped[:].rearrange("p u r -> p r u"))
+
+        bias_flipped = bank_pool.tile([P, P], BF16, name="bias_flipped", tag="bank")
+        nc.tensor.transpose(bias_flipped[:], bias_rows[:], ident_bf[:])
+        bias_cols = const.tile([P, P], F32, name="bias_cols")
+        nc.scalar.copy(out=bias_cols[:], in_=bias_flipped[:])
+        b2_flipped = bank_pool.tile([P, P], BF16, name="b2_flipped", tag="bank")
+        nc.tensor.transpose(b2_flipped[:], b2_rows[:], ident_bf[:])
+        b2_col = const.tile([P, 1], F32, name="b2_col")
+        nc.scalar.copy(out=b2_col[:], in_=b2_flipped[:, 0:1])
 
         pair_codes = {}
         pair_scales = {}
 
         def quantise_tokens(s):
-            words = token_words[s]
-            for side in ("j", "i"):
+            grouped = token_grouped[s]
+            for side in SIDES:
                 pair_codes[s, side] = const.tile(
-                    [P, PAIRS], U32, name="codes_%s_%s" % (s, side), align_bytes=64
+                    [P, PAIRS], U32, name="pair_codes_%s_%s" % (s, side), align_bytes=64
                 )
                 pair_scales[s, side] = const.tile(
-                    [P, PAIRS], U8, name="scales_%s_%s" % (s, side), align_bytes=64
+                    [P, PAIRS], U8, name="pair_scales_%s_%s" % (s, side), align_bytes=64
                 )
-            codes = const.tile([P, TOKENS], U32, name="codes_" + s, align_bytes=64)
-            scales = const.tile([P, TOKENS], U8, name="scales_" + s, align_bytes=64)
+            token_codes = const.tile([P, TOKENS], U32, name="token_codes_" + s, align_bytes=64)
+            token_scales = const.tile([P, TOKENS], U8, name="token_scales_" + s, align_bytes=64)
             fourfold = stage.tile([P, TOKENS, WORD, PACK], BF16, name="fourfold", align_bytes=64)
-            codes_fourfold = stage.tile([P, TOKENS * WORD], U32, name="codes_fourfold", align_bytes=64)
-            scales_fourfold = const.tile([P, TOKENS * WORD], U8, name="scales4_" + s, align_bytes=64)
-            nc.vector.memset(scales[:].bitcast(I32), 0)
-            nc.vector.memset(scales_fourfold[:].bitcast(I32), 0)
+            fourfold_codes = stage.tile(
+                [P, TOKENS * WORD], U32, name="fourfold_codes", align_bytes=64
+            )
+            fourfold_scales = stage.tile(
+                [P, TOKENS * WORD], U8, name="fourfold_scales", align_bytes=64
+            )
+            nc.vector.memset(token_scales[:].bitcast(I32), 0)
+            nc.vector.memset(fourfold_scales[:].bitcast(I32), 0)
             nc.vector.tensor_copy(
-                out=fourfold[:], in_=words[:].unsqueeze(2).to_broadcast([P, TOKENS, WORD, PACK])
+                out=fourfold[:], in_=grouped[:].unsqueeze(2).to_broadcast([P, TOKENS, WORD, PACK])
             )
             nc.vector.quantize_mx(
-                out=codes[:].bitcast(FP8X4),
-                scales=scales[:],
-                in_=words[:].rearrange("p r u -> p (r u)"),
+                out=token_codes[:].bitcast(FP8X4),
+                scales=token_scales[:],
+                in_=grouped[:].rearrange("p r u -> p (r u)"),
             )
             nc.vector.quantize_mx(
-                out=codes_fourfold[:].bitcast(FP8X4),
-                scales=scales_fourfold[:],
+                out=fourfold_codes[:].bitcast(FP8X4),
+                scales=fourfold_scales[:],
                 in_=fourfold[:].rearrange("p r f u -> p (r f u)"),
             )
             nc.vector.tensor_copy(
                 out=pair_codes[s, "j"][:].bitcast(I32).rearrange("p (b i j) -> p b i j", b=B, i=L),
-                in_=codes[:]
+                in_=token_codes[:]
                 .bitcast(I32)
                 .rearrange("p (b j) -> p b j", b=B)
                 .unsqueeze(2)
@@ -153,7 +169,7 @@ def tile_stateencoder_pa_k_kernel(
             )
             nc.vector.tensor_copy(
                 out=pair_scales[s, "j"][:].bitcast(I32).rearrange("p (b i w) -> p b i w", b=B, i=L),
-                in_=scales[:]
+                in_=token_scales[:]
                 .bitcast(I32)
                 .rearrange("p (b w) -> p b w", b=B)
                 .unsqueeze(2)
@@ -161,24 +177,18 @@ def tile_stateencoder_pa_k_kernel(
             )
             nc.vector.tensor_copy(
                 out=pair_codes[s, "i"][:].bitcast(I32).rearrange("p (r j) -> p r j", j=L),
-                in_=codes[:].bitcast(I32).unsqueeze(2).to_broadcast([P, TOKENS, L]),
+                in_=token_codes[:].bitcast(I32).unsqueeze(2).to_broadcast([P, TOKENS, L]),
             )
             nc.vector.tensor_copy(
                 out=pair_scales[s, "i"][:].bitcast(I32).rearrange("p (r w) -> p r w", w=L // WORD),
-                in_=scales_fourfold[:].bitcast(I32).unsqueeze(2).to_broadcast([P, TOKENS, L // WORD]),
+                in_=fourfold_scales[:]
+                .bitcast(I32)
+                .unsqueeze(2)
+                .to_broadcast([P, TOKENS, L // WORD]),
             )
 
         for s in STREAMS:
             quantise_tokens(s)
-
-        bias_flipped = bank_pool.tile([P, P], BF16, name="bias_flipped", tag="bank")
-        nc.tensor.transpose(bias_flipped[:], bias_rows[:], ident_bf[:])
-        bias_cols = const.tile([P, P], F32, name="bias_cols")
-        nc.vector.tensor_copy(out=bias_cols[:], in_=bias_flipped[:])
-        b2_flipped = bank_pool.tile([P, P], BF16, name="b2_flipped", tag="bank")
-        nc.tensor.transpose(b2_flipped[:], b2_rows[:], ident_bf[:])
-        b2_col = const.tile([P, 1], F32, name="b2_col")
-        nc.vector.tensor_copy(out=b2_col[:], in_=b2_flipped[:, 0:1])
 
         mix = const.tile([P, 2], F32, name="mix")
         nc.vector.tensor_copy(out=mix[:], in_=mix_bf[:])
@@ -203,27 +213,33 @@ def tile_stateencoder_pa_k_kernel(
         nc.vector.tensor_mul(out=gain_sp[:], in0=weight_sp[:], in1=gain[:])
 
         grouped_pieces = {}
-        weight_words = {}
+        grouped_w2 = {}
+        weight_operands = {}
 
         def regroup_piece(m):
             g, piece = divmod(m, PIECES)
             s, half = STREAMS[piece // HALVES], piece % HALVES
+            half_rows = slice(half * PACK, (half + 1) * PACK)
             grouped = grouped_pool.tile([P, K_PASS, PACK], BF16, name="grouped", align_bytes=64)
-            rows = slice(half * PACK, (half + 1) * PACK)
             split = K_PASS - SCALAR_COLUMNS
-            for copy, cols in (
+            for copy, share in (
                 (nc.vector.tensor_copy, slice(0, split)),
                 (nc.scalar.copy, slice(split, K_PASS)),
             ):
                 copy(
-                    out=grouped[:, cols, :].rearrange("p (c i) u -> p c u i", i=4),
-                    in_=raw_groups[g][s][:, rows, cols].rearrange("p u (c i) -> p c u i", i=4),
+                    out=grouped[:, share, :].rearrange("p (c i) u -> p c u i", i=RUN),
+                    in_=raw_groups[g][s][:, half_rows, share].rearrange(
+                        "p u (c i) -> p c u i", i=RUN
+                    ),
                 )
             grouped_pieces[m] = grouped
             if piece == 0:
-                grouped2 = grouped_pool.tile([P, OUT, PACK], BF16, name="grouped2", align_bytes=64)
-                nc.scalar.copy(out=grouped2[:], in_=raw_groups[g]["W2"][:].rearrange("p t o -> p o t"))
-                grouped_pieces["W2", g] = grouped2
+                grouped_w2[g] = grouped_pool.tile(
+                    [P, OUT, PACK], BF16, name="grouped_w2", align_bytes=64
+                )
+                nc.scalar.copy(
+                    out=grouped_w2[g][:], in_=raw_groups[g]["W2"][:].rearrange("p t o -> p o t")
+                )
             if piece == PIECES - 1 and g + 2 < GROUPS:
                 load_group(g + 2)
 
@@ -231,55 +247,55 @@ def tile_stateencoder_pa_k_kernel(
             g, piece = divmod(m, PIECES)
             s, half = STREAMS[piece // HALVES], piece % HALVES
             if half == 0:
-                weight_words[g, s] = (
+                weight_operands[g, s] = (
                     weight_pool.tile([P, HALVES, K_PASS], U32, name="w_codes_" + s, align_bytes=64),
                     weight_pool.tile([P, HALVES, K_PASS], U8, name="w_scales_" + s, align_bytes=64),
                 )
-            codes, scales = weight_words[g, s]
+            w_codes, w_scales = weight_operands[g, s]
             nc.vector.quantize_mx(
-                out=codes[:, half, :].bitcast(FP8X4),
-                scales=scales[:, half, :],
+                out=w_codes[:, half, :].bitcast(FP8X4),
+                scales=w_scales[:, half, :],
                 in_=grouped_pieces[m][:].rearrange("p w u -> p (w u)"),
             )
             if piece == 0:
-                codes2 = weight_pool.tile([P, OUT], U32, name="w2_codes", bufs=4, align_bytes=64)
-                scales2 = weight_pool.tile([P, OUT], U8, name="w2_scales", bufs=4, align_bytes=64)
+                w2_codes = weight_pool.tile([P, OUT], U32, name="w2_codes", bufs=4, align_bytes=64)
+                w2_scales = weight_pool.tile([P, OUT], U8, name="w2_scales", bufs=4, align_bytes=64)
                 nc.vector.quantize_mx(
-                    out=codes2[:].bitcast(FP8X4),
-                    scales=scales2[:],
-                    in_=grouped_pieces["W2", g][:].rearrange("p o t -> p (o t)"),
+                    out=w2_codes[:].bitcast(FP8X4),
+                    scales=w2_scales[:],
+                    in_=grouped_w2[g][:].rearrange("p o t -> p (o t)"),
                 )
-                weight_words[g, "W2"] = (codes2, scales2)
+                weight_operands[g, "W2"] = (w2_codes, w2_scales)
 
         def regroup_beside(unit):
-            if unit + LEAD + 1 < GROUPS * PIECES:
+            if unit + LEAD + 1 < ALL_PIECES:
                 regroup_piece(unit + LEAD + 1)
 
         def quantise_beside(unit):
-            if 0 <= unit + LEAD < GROUPS * PIECES:
+            if 0 <= unit + LEAD < ALL_PIECES:
                 quantise_piece(unit + LEAD)
 
         acc = [acc_pool.tile([P, BANK], F32, name="acc%d" % blk) for blk in range(BLOCKS)]
         hidden_tiles = {}
         state_tiles = {}
-        state_words = {}
+        state_operands = {}
 
         def first_stage(unit):
             g, blk = divmod(unit, BLOCKS)
-            cols = slice(blk * BANK, (blk + 1) * BANK)
+            pair_range = slice(blk * BANK, (blk + 1) * BANK)
             for s in STREAMS:
-                codes, scales = weight_words[g, s]
+                w_codes, w_scales = weight_operands[g, s]
                 hidden = hidden_pool.tile([P, PACK, BANK], F32, name="hidden_" + s)
                 for t in range(PACK):
-                    units = slice(t * P, (t + 1) * P)
+                    chunk = slice(t * P, (t + 1) * P)
                     bank = bank_pool.tile([P, BANK], F32, name="bank", tag="bank")
-                    for half, side in enumerate(("j", "i")):
+                    for half, side in enumerate(SIDES):
                         nc.tensor.matmul_mx(
                             out=bank[:],
-                            lhsT=codes[:, half, units].bitcast(FP8X4),
-                            lhsT_scale=scales[:, half, units],
-                            rhs=pair_codes[s, side][:, cols].bitcast(FP8X4),
-                            rhs_scale=pair_scales[s, side][:, cols],
+                            lhsT=w_codes[:, half, chunk].bitcast(FP8X4),
+                            lhsT_scale=w_scales[:, half, chunk],
+                            rhs=pair_codes[s, side][:, pair_range].bitcast(FP8X4),
+                            rhs_scale=pair_scales[s, side][:, pair_range],
                             start=(half == 0),
                             stop=(half == HALVES - 1),
                         )
@@ -307,8 +323,8 @@ def tile_stateencoder_pa_k_kernel(
         def round_state(unit):
             state = state_pool.tile([P, BANK, PACK], BF16, name="state", bufs=2, align_bytes=64)
             nc.vector.tensor_scalar(
-                out=state[:].rearrange("p (c i) t -> p c t i", i=4),
-                in0=hidden_tiles[unit, "utt"][:].rearrange("p t (c i) -> p c t i", i=4),
+                out=state[:].rearrange("p (c i) t -> p c t i", i=RUN),
+                in0=hidden_tiles[unit, "utt"][:].rearrange("p t (c i) -> p c t i", i=RUN),
                 scalar1=gain_sp[:, 0:1],
                 scalar2=None,
                 op0=ALU.mult,
@@ -316,14 +332,14 @@ def tile_stateencoder_pa_k_kernel(
             state_tiles[unit] = state
 
         def quantise_state(unit):
-            codes = state_pool.tile([P, BANK], U32, name="state_codes", align_bytes=64)
-            scales = state_pool.tile([P, BANK], U8, name="state_scales", align_bytes=64)
+            state_codes = state_pool.tile([P, BANK], U32, name="state_codes", align_bytes=64)
+            state_scales = state_pool.tile([P, BANK], U8, name="state_scales", align_bytes=64)
             nc.vector.quantize_mx(
-                out=codes[:].bitcast(FP8X4),
-                scales=scales[:],
+                out=state_codes[:].bitcast(FP8X4),
+                scales=state_scales[:],
                 in_=state_tiles[unit][:].rearrange("p c t -> p (c t)"),
             )
-            state_words[unit] = (codes, scales)
+            state_operands[unit] = (state_codes, state_scales)
 
         out_rows = out.rearrange("b i j o -> (b i j) o")
 
@@ -335,23 +351,23 @@ def tile_stateencoder_pa_k_kernel(
             turned = bank_pool.tile([P, BANK // P, OUT], F32, name="turned", tag="bank")
             for r in range(BANK // P):
                 nc.tensor.transpose(turned[:, r, :], result[:, r * P : (r + 1) * P], ident_f32[:])
-            rows_out = result_pool.tile([P, BANK // P, OUT], F32, name="rows_out")
-            nc.vector.tensor_copy(out=rows_out[:], in_=turned[:])
+            result_rows = result_pool.tile([P, BANK // P, OUT], F32, name="result_rows")
+            nc.scalar.copy(out=result_rows[:], in_=turned[:])
             nc.sync.dma_start(
                 out=out_rows[blk * BANK : (blk + 1) * BANK, :].rearrange("(r p) o -> p r o", p=P),
-                in_=rows_out[:],
+                in_=result_rows[:],
             )
 
         def second_stage(unit):
             g, blk = divmod(unit, BLOCKS)
-            codes2, scales2 = weight_words[g, "W2"]
-            codes, scales = state_words[unit]
+            w2_codes, w2_scales = weight_operands[g, "W2"]
+            state_codes, state_scales = state_operands[unit]
             nc.tensor.matmul_mx(
                 out=acc[blk][:],
-                lhsT=codes2[:].bitcast(FP8X4),
-                lhsT_scale=scales2[:],
-                rhs=codes[:].bitcast(FP8X4),
-                rhs_scale=scales[:],
+                lhsT=w2_codes[:].bitcast(FP8X4),
+                lhsT_scale=w2_scales[:],
+                rhs=state_codes[:].bitcast(FP8X4),
+                rhs_scale=state_scales[:],
                 start=(g == 0),
                 stop=(g == GROUPS - 1),
             )

@@ -22,16 +22,21 @@ TOKENS = B * L
 PAIRS = B * L * L
 BANK = 512
 BLOCKS = PAIRS // BANK
+ROWS = L // BLOCKS
 GROUPS = H // K_PASS
 UNITS = GROUPS * BLOCKS
+W2_SET = 4
+SET_UNITS = W2_SET * BLOCKS
 STREAMS = ("sp", "utt")
 SIDES = ("j", "i")
 HALVES = len(SIDES)
 PIECES = len(STREAMS) * HALVES
 ALL_PIECES = GROUPS * PIECES
 LAG = 2
-LEAD = PIECES + LAG
-SCALAR_COLUMNS = 128
+LEAD = PIECES + 1
+SCALAR_COLUMNS = 192
+SCALAR_PIECES = (0, 2)
+VECTOR_PIECES = (1, 3, 4, 5)
 MAX_LOGIT_GAP = 40.0
 
 FLOPS = 4 * 2 * TOKENS * D * H + 2 * PAIRS * H * OUT
@@ -58,52 +63,64 @@ def tile_stateencoder_pa_k_kernel(
         acc_pool = ctx.enter_context(tc.psum_pool(name="acc", bufs=1))
         bank_pool = ctx.enter_context(tc.psum_pool(name="bank", bufs=4))
 
+        warm = const.tile([P, 1], F32, name="warm")
+        nc.vector.memset(warm[:], 0.0)
+        warm_out = const.tile([P, 1], F32, name="warm_out")
+        nc.scalar.activation(out=warm_out[:], in_=warm[:], func=ACT.Exp)
+
+        b2_rows = const.tile([P, P], BF16, name="b2_rows")
+        nc.gpsimd.memset(b2_rows[:], 0.0)
         ident_bf = const.tile([P, P], BF16, name="ident_bf")
         masks.make_identity(nc, ident_bf[:])
-        ident_f32 = const.tile([P, P], F32, name="ident_f32")
-        masks.make_identity(nc, ident_f32[:])
 
         raw_groups = {}
 
-        def load_group(g):
+        def load_weights(g, s, pieces):
             hidden_range = slice(g * K_PASS, (g + 1) * K_PASS)
-            raws = {}
-            raws["W2"] = raw_pool.tile([P, PACK, OUT], BF16, name="raw_w2")
+            raw = raw_pool.tile([P, HALVES * PACK, K_PASS], BF16, name="raw_" + s, tag="raw_w")
+            rows = weights_dram[s][:, hidden_range].rearrange("(v q) w -> q v w", q=P)
+            step = HALVES * PACK // pieces
+            for v in range(0, HALVES * PACK, step):
+                nc.sync.dma_start(out=raw[:, v : v + step, :], in_=rows[:, v : v + step, :])
+            raw_groups[g, s] = raw
+
+        def load_w2(q):
+            raw = raw_pool.tile([P, W2_SET * PACK, OUT], BF16, name="raw_w2", bufs=2)
+            w2_rows = W2_SET * K_PASS
             nc.sync.dma_start(
-                out=raws["W2"][:], in_=W2[hidden_range, :].rearrange("(t p) o -> p t o", p=P)
+                out=raw[:],
+                in_=W2[q * w2_rows : (q + 1) * w2_rows, :].rearrange("(v p) o -> p v o", p=P),
             )
-            for s in STREAMS:
-                raws[s] = raw_pool.tile(
-                    [P, HALVES * PACK, K_PASS], BF16, name="raw_" + s, tag="raw_w"
-                )
-                nc.sync.dma_start(
-                    out=raws[s][:],
-                    in_=weights_dram[s][:, hidden_range].rearrange("(v q) w -> q v w", q=P),
-                )
-            raw_groups[g] = raws
+            raw_groups[q, "W2"] = raw
 
         token_rows = {}
-        for s in STREAMS:
+
+        def load_tokens(s):
             token_rows[s] = const.tile([P, D], BF16, name="token_rows_" + s)
             nc.sync.dma_start(
                 out=token_rows[s][:], in_=tokens_dram[s].rearrange("b l d -> (b l) d")
             )
-        load_group(0)
-        load_group(1)
+
+        for s in STREAMS:
+            load_tokens(s)
+            load_weights(0, s, HALVES)
 
         bias_rows = const.tile([P, P], BF16, name="bias_rows")
-        nc.scalar.dma_start(out=bias_rows[0 : H // P, :], in_=b_utt.rearrange("(c p) -> c p", p=P))
-        nc.scalar.dma_start(out=bias_rows[H // P : P, :], in_=b_sp.rearrange("(c p) -> c p", p=P))
+        nc.sync.dma_start(out=bias_rows[0 : H // P, :], in_=b_utt.rearrange("(c p) -> c p", p=P))
+        nc.sync.dma_start(out=bias_rows[H // P : P, :], in_=b_sp.rearrange("(c p) -> c p", p=P))
+        nc.sync.dma_start(out=b2_rows[0:1, :], in_=b2.rearrange("(r c) -> r c", r=1))
         mix_bf = const.tile([P, 2], BF16, name="mix_bf")
-        nc.scalar.dma_start(out=mix_bf[:], in_=mix_w.partition_broadcast(P))
+        nc.sync.dma_start(out=mix_bf[:], in_=mix_w.partition_broadcast(P))
         gamma_bf = const.tile([P, 1], BF16, name="gamma_bf")
-        nc.scalar.dma_start(out=gamma_bf[:], in_=gamma.partition_broadcast(P))
-        b2_rows = const.tile([P, P], BF16, name="b2_rows")
-        nc.vector.memset(b2_rows[:], 0.0)
-        nc.scalar.dma_start(out=b2_rows[0:1, :], in_=b2.rearrange("(r c) -> r c", r=1))
+        nc.sync.dma_start(out=gamma_bf[:], in_=gamma.partition_broadcast(P))
+        load_w2(0)
+        for s in STREAMS:
+            load_weights(1, s, 1)
+
 
         token_grouped = {}
-        for s in STREAMS:
+
+        def turn_tokens(s):
             flipped = bank_pool.tile([P, PACK, TOKENS], BF16, name="flipped", tag="bank")
             for u in range(PACK):
                 nc.tensor.transpose(
@@ -112,40 +129,57 @@ def tile_stateencoder_pa_k_kernel(
             token_grouped[s] = const.tile(
                 [P, TOKENS, PACK], BF16, name="token_grouped_" + s, align_bytes=64
             )
-            nc.scalar.copy(out=token_grouped[s][:], in_=flipped[:].rearrange("p u r -> p r u"))
+            copy = nc.vector.tensor_copy if s == STREAMS[0] else nc.scalar.copy
+            copy(out=token_grouped[s][:], in_=flipped[:].rearrange("p u r -> p r u"))
 
-        bias_flipped = bank_pool.tile([P, P], BF16, name="bias_flipped", tag="bank")
-        nc.tensor.transpose(bias_flipped[:], bias_rows[:], ident_bf[:])
         bias_cols = const.tile([P, P], F32, name="bias_cols")
-        nc.scalar.copy(out=bias_cols[:], in_=bias_flipped[:])
-        b2_flipped = bank_pool.tile([P, P], BF16, name="b2_flipped", tag="bank")
-        nc.tensor.transpose(b2_flipped[:], b2_rows[:], ident_bf[:])
         b2_col = const.tile([P, 1], F32, name="b2_col")
-        nc.scalar.copy(out=b2_col[:], in_=b2_flipped[:, 0:1])
+
+        def turn_biases():
+            bias_flipped = bank_pool.tile([P, P], BF16, name="bias_flipped", tag="bank")
+            nc.tensor.transpose(bias_flipped[:], bias_rows[:], ident_bf[:])
+            nc.scalar.copy(out=bias_cols[:], in_=bias_flipped[:])
+            b2_flipped = bank_pool.tile([P, P], BF16, name="b2_flipped", tag="bank")
+            nc.tensor.transpose(b2_flipped[:], b2_rows[:], ident_bf[:])
+            nc.scalar.copy(out=b2_col[:], in_=b2_flipped[:, 0:1])
 
         pair_codes = {}
         pair_scales = {}
+        side_columns = {"j": BANK, "i": PAIRS}
+        token_planes = {}
+        for s in STREAMS:
+            for side in SIDES:
+                pair_codes[s, side] = const.tile(
+                    [P, side_columns[side]],
+                    U32,
+                    name="pair_codes_%s_%s" % (s, side),
+                    align_bytes=64,
+                )
+                pair_scales[s, side] = const.tile(
+                    [P, side_columns[side]],
+                    U8,
+                    name="pair_scales_%s_%s" % (s, side),
+                    align_bytes=64,
+                )
+            token_scales = const.tile([P, TOKENS], U8, name="token_scales_" + s, align_bytes=64)
+            nc.gpsimd.memset(token_scales[:].bitcast(I32), 0)
+            fourfold_scales = const.tile(
+                [P, TOKENS * WORD], U8, name="fourfold_scales_" + s, align_bytes=64
+            )
+            nc.gpsimd.memset(fourfold_scales[:].bitcast(I32), 0)
+            token_codes = const.tile([P, TOKENS], U32, name="token_codes_" + s, align_bytes=64)
+            token_planes[s] = (token_codes, token_scales, fourfold_scales)
+
+        ident_f32 = const.tile([P, P], F32, name="ident_f32")
+        masks.make_identity(nc, ident_f32[:])
 
         def quantise_tokens(s):
             grouped = token_grouped[s]
-            for side in SIDES:
-                pair_codes[s, side] = const.tile(
-                    [P, PAIRS], U32, name="pair_codes_%s_%s" % (s, side), align_bytes=64
-                )
-                pair_scales[s, side] = const.tile(
-                    [P, PAIRS], U8, name="pair_scales_%s_%s" % (s, side), align_bytes=64
-                )
-            token_codes = const.tile([P, TOKENS], U32, name="token_codes_" + s, align_bytes=64)
-            token_scales = const.tile([P, TOKENS], U8, name="token_scales_" + s, align_bytes=64)
+            token_codes, token_scales, fourfold_scales = token_planes[s]
             fourfold = stage.tile([P, TOKENS, WORD, PACK], BF16, name="fourfold", align_bytes=64)
             fourfold_codes = stage.tile(
                 [P, TOKENS * WORD], U32, name="fourfold_codes", align_bytes=64
             )
-            fourfold_scales = stage.tile(
-                [P, TOKENS * WORD], U8, name="fourfold_scales", align_bytes=64
-            )
-            nc.vector.memset(token_scales[:].bitcast(I32), 0)
-            nc.vector.memset(fourfold_scales[:].bitcast(I32), 0)
             nc.vector.tensor_copy(
                 out=fourfold[:], in_=grouped[:].unsqueeze(2).to_broadcast([P, TOKENS, WORD, PACK])
             )
@@ -160,59 +194,68 @@ def tile_stateencoder_pa_k_kernel(
                 in_=fourfold[:].rearrange("p r f u -> p (r f u)"),
             )
             nc.vector.tensor_copy(
-                out=pair_codes[s, "j"][:].bitcast(I32).rearrange("p (b i j) -> p b i j", b=B, i=L),
+                out=pair_codes[s, "j"][:]
+                .bitcast(I32)
+                .rearrange("p (b i j) -> p b i j", b=B, i=ROWS),
                 in_=token_codes[:]
                 .bitcast(I32)
                 .rearrange("p (b j) -> p b j", b=B)
                 .unsqueeze(2)
-                .to_broadcast([P, B, L, L]),
+                .to_broadcast([P, B, ROWS, L]),
             )
             nc.vector.tensor_copy(
-                out=pair_scales[s, "j"][:].bitcast(I32).rearrange("p (b i w) -> p b i w", b=B, i=L),
+                out=pair_scales[s, "j"][:]
+                .bitcast(I32)
+                .rearrange("p (b i w) -> p b i w", b=B, i=ROWS),
                 in_=token_scales[:]
                 .bitcast(I32)
                 .rearrange("p (b w) -> p b w", b=B)
                 .unsqueeze(2)
-                .to_broadcast([P, B, L, L // WORD]),
-            )
-            nc.vector.tensor_copy(
-                out=pair_codes[s, "i"][:].bitcast(I32).rearrange("p (r j) -> p r j", j=L),
-                in_=token_codes[:].bitcast(I32).unsqueeze(2).to_broadcast([P, TOKENS, L]),
-            )
-            nc.vector.tensor_copy(
-                out=pair_scales[s, "i"][:].bitcast(I32).rearrange("p (r w) -> p r w", w=L // WORD),
-                in_=fourfold_scales[:]
-                .bitcast(I32)
-                .unsqueeze(2)
-                .to_broadcast([P, TOKENS, L // WORD]),
+                .to_broadcast([P, B, ROWS, L // WORD]),
             )
 
-        for s in STREAMS:
-            quantise_tokens(s)
+        def repeat_side_i(s, first, last):
+            token_codes, token_scales, fourfold_scales = token_planes[s]
+            for plane, repeated, words in (
+                (token_codes, pair_codes[s, "i"], L),
+                (fourfold_scales, pair_scales[s, "i"], L // WORD),
+            ):
+                nc.vector.tensor_copy(
+                    out=repeated[:, first * BANK : last * BANK]
+                    .bitcast(I32)
+                    .rearrange("p (k b i w) -> p b k i w", k=last - first, b=B, i=ROWS),
+                    in_=plane[:]
+                    .bitcast(I32)
+                    .rearrange("p (b k i) -> p b k i", b=B, i=ROWS)[:, :, first:last, :]
+                    .unsqueeze(4)
+                    .to_broadcast([P, B, last - first, ROWS, words]),
+                )
 
         mix = const.tile([P, 2], F32, name="mix")
-        nc.vector.tensor_copy(out=mix[:], in_=mix_bf[:])
         gain = const.tile([P, 1], F32, name="gain")
-        nc.vector.tensor_copy(out=gain[:], in_=gamma_bf[:])
         gap = const.tile([P, 1], F32, name="gap")
-        nc.vector.tensor_scalar(
-            out=gap[:],
-            in0=mix[:, 0:1],
-            scalar1=mix[:, 1:2],
-            scalar2=MAX_LOGIT_GAP,
-            op0=ALU.subtract,
-            op1=ALU.min,
-        )
         ratio = const.tile([P, 1], F32, name="ratio")
-        nc.scalar.activation(out=ratio[:], in_=gap[:], func=ACT.Exp)
         denominator = const.tile([P, 1], F32, name="denominator")
-        nc.vector.tensor_scalar_add(out=denominator[:], in0=ratio[:], scalar1=1.0)
         weight_sp = const.tile([P, 1], F32, name="weight_sp")
-        nc.vector.reciprocal(out=weight_sp[:], in_=denominator[:])
         gain_sp = const.tile([P, 1], F32, name="gain_sp")
-        nc.vector.tensor_mul(out=gain_sp[:], in0=weight_sp[:], in1=gain[:])
 
-        grouped_pieces = {}
+        def mix_weights():
+            nc.gpsimd.tensor_copy(out=mix[:], in_=mix_bf[:])
+            nc.gpsimd.tensor_copy(out=gain[:], in_=gamma_bf[:])
+            nc.gpsimd.tensor_scalar(
+                out=gap[:],
+                in0=mix[:, 0:1],
+                scalar1=mix[:, 1:2],
+                scalar2=MAX_LOGIT_GAP,
+                op0=ALU.subtract,
+                op1=ALU.min,
+            )
+            nc.scalar.activation(out=ratio[:], in_=gap[:], func=ACT.Exp)
+            nc.gpsimd.tensor_scalar_add(out=denominator[:], in0=ratio[:], scalar1=1.0)
+            nc.vector.reciprocal(out=weight_sp[:], in_=denominator[:])
+            nc.gpsimd.tensor_mul(out=gain_sp[:], in0=weight_sp[:], in1=gain[:])
+
+        grouped_weights = {}
         grouped_w2 = {}
         weight_operands = {}
 
@@ -220,60 +263,78 @@ def tile_stateencoder_pa_k_kernel(
             g, piece = divmod(m, PIECES)
             s, half = STREAMS[piece // HALVES], piece % HALVES
             half_rows = slice(half * PACK, (half + 1) * PACK)
-            grouped = grouped_pool.tile([P, K_PASS, PACK], BF16, name="grouped", align_bytes=64)
-            split = K_PASS - SCALAR_COLUMNS
+            if half == 0:
+                grouped_weights[g, s] = grouped_pool.tile(
+                    [P, HALVES, K_PASS, PACK], BF16, name="grouped", align_bytes=64
+                )
+            grouped = grouped_weights[g, s]
+            if m in SCALAR_PIECES:
+                split = 0
+            elif m in VECTOR_PIECES:
+                split = K_PASS
+            else:
+                split = K_PASS - SCALAR_COLUMNS
             for copy, share in (
                 (nc.vector.tensor_copy, slice(0, split)),
                 (nc.scalar.copy, slice(split, K_PASS)),
             ):
-                copy(
-                    out=grouped[:, share, :].rearrange("p (c i) u -> p c u i", i=RUN),
-                    in_=raw_groups[g][s][:, half_rows, share].rearrange(
-                        "p u (c i) -> p c u i", i=RUN
-                    ),
-                )
-            grouped_pieces[m] = grouped
-            if piece == 0:
-                grouped_w2[g] = grouped_pool.tile(
-                    [P, OUT, PACK], BF16, name="grouped_w2", align_bytes=64
-                )
-                nc.scalar.copy(
-                    out=grouped_w2[g][:], in_=raw_groups[g]["W2"][:].rearrange("p t o -> p o t")
-                )
-            if piece == PIECES - 1 and g + 2 < GROUPS:
-                load_group(g + 2)
+                if share.start < share.stop:
+                    copy(
+                        out=grouped[:, half, share, :].rearrange("p (c i) u -> p c u i", i=RUN),
+                        in_=raw_groups[g, s][:, half_rows, share].rearrange(
+                            "p u (c i) -> p c u i", i=RUN
+                        ),
+                    )
+            if half == HALVES - 1 and g + 2 < GROUPS:
+                load_weights(g + 2, s, 1)
 
-        def quantise_piece(m):
-            g, piece = divmod(m, PIECES)
-            s, half = STREAMS[piece // HALVES], piece % HALVES
-            if half == 0:
+        def quantise_weights(g, s, halves):
+            first, last = halves
+            if first == 0:
                 weight_operands[g, s] = (
                     weight_pool.tile([P, HALVES, K_PASS], U32, name="w_codes_" + s, align_bytes=64),
                     weight_pool.tile([P, HALVES, K_PASS], U8, name="w_scales_" + s, align_bytes=64),
                 )
             w_codes, w_scales = weight_operands[g, s]
             nc.vector.quantize_mx(
-                out=w_codes[:, half, :].bitcast(FP8X4),
-                scales=w_scales[:, half, :],
-                in_=grouped_pieces[m][:].rearrange("p w u -> p (w u)"),
+                out=w_codes[:, first:last, :].rearrange("p h w -> p (h w)").bitcast(FP8X4),
+                scales=w_scales[:, first:last, :].rearrange("p h w -> p (h w)"),
+                in_=grouped_weights[g, s][:, first:last, :, :].rearrange("p h w u -> p (h w u)"),
             )
-            if piece == 0:
-                w2_codes = weight_pool.tile([P, OUT], U32, name="w2_codes", bufs=4, align_bytes=64)
-                w2_scales = weight_pool.tile([P, OUT], U8, name="w2_scales", bufs=4, align_bytes=64)
-                nc.vector.quantize_mx(
-                    out=w2_codes[:].bitcast(FP8X4),
-                    scales=w2_scales[:],
-                    in_=grouped_w2[g][:].rearrange("p o t -> p (o t)"),
+
+        def regroup_w2(q, copy, first, last):
+            if first == 0:
+                grouped_w2[q] = grouped_pool.tile(
+                    [P, W2_SET, OUT, PACK], BF16, name="grouped_w2", bufs=1, align_bytes=64
                 )
-                weight_operands[g, "W2"] = (w2_codes, w2_scales)
+            copy(
+                out=grouped_w2[q][:, first:last, :, :],
+                in_=raw_groups[q, "W2"][:, first * PACK : last * PACK, :].rearrange(
+                    "p (g t) o -> p g o t", t=PACK
+                ),
+            )
+            if last == W2_SET and (q + 1) * W2_SET < GROUPS:
+                load_w2(q + 1)
+
+        def quantise_w2(q):
+            w2_codes = weight_pool.tile([P, W2_SET, OUT], U32, name="w2_codes", bufs=2, align_bytes=64)
+            w2_scales = weight_pool.tile([P, W2_SET, OUT], U8, name="w2_scales", bufs=2, align_bytes=64)
+            nc.vector.quantize_mx(
+                out=w2_codes[:].rearrange("p g o -> p (g o)").bitcast(FP8X4),
+                scales=w2_scales[:].rearrange("p g o -> p (g o)"),
+                in_=grouped_w2[q][:].rearrange("p g o t -> p (g o t)"),
+            )
+            for i in range(W2_SET):
+                weight_operands[q * W2_SET + i, "W2"] = (w2_codes[:, i, :], w2_scales[:, i, :])
 
         def regroup_beside(unit):
             if unit + LEAD + 1 < ALL_PIECES:
                 regroup_piece(unit + LEAD + 1)
 
         def quantise_beside(unit):
-            if 0 <= unit + LEAD < ALL_PIECES:
-                quantise_piece(unit + LEAD)
+            g, piece = divmod(unit + LEAD, PIECES)
+            if unit + LEAD < ALL_PIECES and piece % HALVES == HALVES - 1:
+                quantise_weights(g, STREAMS[piece // HALVES], (0, HALVES))
 
         acc = [acc_pool.tile([P, BANK], F32, name="acc%d" % blk) for blk in range(BLOCKS)]
         hidden_tiles = {}
@@ -282,7 +343,7 @@ def tile_stateencoder_pa_k_kernel(
 
         def first_stage(unit):
             g, blk = divmod(unit, BLOCKS)
-            pair_range = slice(blk * BANK, (blk + 1) * BANK)
+            side_range = {"j": slice(0, BANK), "i": slice(blk * BANK, (blk + 1) * BANK)}
             for s in STREAMS:
                 w_codes, w_scales = weight_operands[g, s]
                 hidden = hidden_pool.tile([P, PACK, BANK], F32, name="hidden_" + s)
@@ -294,8 +355,8 @@ def tile_stateencoder_pa_k_kernel(
                             out=bank[:],
                             lhsT=w_codes[:, half, chunk].bitcast(FP8X4),
                             lhsT_scale=w_scales[:, half, chunk],
-                            rhs=pair_codes[s, side][:, pair_range].bitcast(FP8X4),
-                            rhs_scale=pair_scales[s, side][:, pair_range],
+                            rhs=pair_codes[s, side][:, side_range[side]].bitcast(FP8X4),
+                            rhs_scale=pair_scales[s, side][:, side_range[side]],
                             start=(half == 0),
                             stop=(half == HALVES - 1),
                         )
@@ -311,14 +372,17 @@ def tile_stateencoder_pa_k_kernel(
 
         def mix_streams(unit):
             hidden_utt = hidden_tiles[unit, "utt"]
-            nc.vector.scalar_tensor_tensor(
-                out=hidden_utt[:],
-                in0=hidden_utt[:],
-                scalar=ratio[:, 0:1],
-                in1=hidden_tiles[unit, "sp"][:],
-                op0=ALU.mult,
-                op1=ALU.add,
-            )
+            step = 1 if unit == UNITS - 1 else PACK
+            for t in range(0, PACK, step):
+                chunks = slice(t, t + step)
+                nc.vector.scalar_tensor_tensor(
+                    out=hidden_utt[:, chunks, :],
+                    in0=hidden_utt[:, chunks, :],
+                    scalar=ratio[:, 0:1],
+                    in1=hidden_tiles[unit, "sp"][:, chunks, :],
+                    op0=ALU.mult,
+                    op1=ALU.add,
+                )
 
         def round_state(unit):
             state = state_pool.tile([P, BANK, PACK], BF16, name="state", bufs=2, align_bytes=64)
@@ -341,7 +405,8 @@ def tile_stateencoder_pa_k_kernel(
             )
             state_operands[unit] = (state_codes, state_scales)
 
-        out_rows = out.rearrange("b i j o -> (b i j) o")
+        PAIR = P // (ROWS * L)
+        out_rows = out.rearrange("(r h) (k i) j o -> k h i j r o", h=PAIR, k=BLOCKS)
 
         def finish_block(blk):
             result = result_pool.tile([P, BANK], F32, name="result")
@@ -353,10 +418,11 @@ def tile_stateencoder_pa_k_kernel(
                 nc.tensor.transpose(turned[:, r, :], result[:, r * P : (r + 1) * P], ident_f32[:])
             result_rows = result_pool.tile([P, BANK // P, OUT], F32, name="result_rows")
             nc.scalar.copy(out=result_rows[:], in_=turned[:])
-            nc.sync.dma_start(
-                out=out_rows[blk * BANK : (blk + 1) * BANK, :].rearrange("(r p) o -> p r o", p=P),
-                in_=result_rows[:],
-            )
+            for h, dma_start in enumerate((nc.sync.dma_start, nc.scalar.dma_start)):
+                dma_start(
+                    out=out_rows[blk, h].rearrange("i j r o -> (i j) r o"),
+                    in_=result_rows[h * ROWS * L : (h + 1) * ROWS * L, :, :],
+                )
 
         def second_stage(unit):
             g, blk = divmod(unit, BLOCKS)
@@ -364,8 +430,8 @@ def tile_stateencoder_pa_k_kernel(
             state_codes, state_scales = state_operands[unit]
             nc.tensor.matmul_mx(
                 out=acc[blk][:],
-                lhsT=w2_codes[:].bitcast(FP8X4),
-                lhsT_scale=w2_scales[:],
+                lhsT=w2_codes.bitcast(FP8X4),
+                lhsT_scale=w2_scales,
                 rhs=state_codes[:].bitcast(FP8X4),
                 rhs_scale=state_scales[:],
                 start=(g == 0),
@@ -374,16 +440,42 @@ def tile_stateencoder_pa_k_kernel(
             if g == GROUPS - 1:
                 finish_block(blk)
 
-        for unit in range(-(LEAD + 1), 0):
-            regroup_beside(unit)
-            quantise_beside(unit)
+        turn_tokens("sp")
+        regroup_piece(0)
+        turn_tokens("utt")
+        quantise_tokens("sp")
+        repeat_side_i("sp", 0, 1)
+        quantise_weights(0, "sp", (0, 1))
+        regroup_piece(1)
+        turn_biases()
+        regroup_piece(2)
+        quantise_weights(0, "sp", (1, 2))
+        quantise_tokens("utt")
+        repeat_side_i("utt", 0, 1)
+        regroup_piece(3)
+        quantise_weights(0, "utt", (0, HALVES))
+        mix_weights()
+        for s in STREAMS:
+            repeat_side_i(s, 1, BLOCKS)
+        regroup_w2(0, nc.vector.tensor_copy, 0, W2_SET)
+        regroup_piece(4)
+        quantise_w2(0)
+        regroup_piece(5)
+
         for unit in range(UNITS + LAG):
             if unit < UNITS:
                 first_stage(unit)
+                q, step = divmod(unit, SET_UNITS)
+                i, blk = divmod(step, BLOCKS)
+                more_w2 = (q + 1) * W2_SET < GROUPS
+                if more_w2 and blk == 1:
+                    regroup_w2(q + 1, nc.scalar.copy, i, i + 1)
                 mix_streams(unit)
                 regroup_beside(unit)
                 round_state(unit)
                 quantise_beside(unit)
+                if more_w2 and step == SET_UNITS - 2:
+                    quantise_w2(q + 1)
                 quantise_state(unit)
             if unit >= LAG:
                 second_stage(unit - LAG)

@@ -255,7 +255,7 @@ def tile_stateencoder_pa_k_kernel(
             nc.vector.reciprocal(out=weight_sp[:], in_=denominator[:])
             nc.gpsimd.tensor_mul(out=gain_sp[:], in0=weight_sp[:], in1=gain[:])
 
-        grouped_weights = {}
+        grouped_pieces = {}
         grouped_w2 = {}
         weight_operands = {}
 
@@ -263,11 +263,8 @@ def tile_stateencoder_pa_k_kernel(
             g, piece = divmod(m, PIECES)
             s, half = STREAMS[piece // HALVES], piece % HALVES
             half_rows = slice(half * PACK, (half + 1) * PACK)
-            if half == 0:
-                grouped_weights[g, s] = grouped_pool.tile(
-                    [P, HALVES, K_PASS, PACK], BF16, name="grouped", align_bytes=64
-                )
-            grouped = grouped_weights[g, s]
+            grouped = grouped_pool.tile([P, K_PASS, PACK], BF16, name="grouped", align_bytes=64)
+            grouped_pieces[m] = grouped
             if m in SCALAR_PIECES:
                 split = 0
             elif m in VECTOR_PIECES:
@@ -280,7 +277,7 @@ def tile_stateencoder_pa_k_kernel(
             ):
                 if share.start < share.stop:
                     copy(
-                        out=grouped[:, half, share, :].rearrange("p (c i) u -> p c u i", i=RUN),
+                        out=grouped[:, share, :].rearrange("p (c i) u -> p c u i", i=RUN),
                         in_=raw_groups[g, s][:, half_rows, share].rearrange(
                             "p u (c i) -> p c u i", i=RUN
                         ),
@@ -288,18 +285,19 @@ def tile_stateencoder_pa_k_kernel(
             if half == HALVES - 1 and g + 2 < GROUPS:
                 load_weights(g + 2, s, 1)
 
-        def quantise_weights(g, s, halves):
-            first, last = halves
-            if first == 0:
+        def quantise_piece(m):
+            g, piece = divmod(m, PIECES)
+            s, half = STREAMS[piece // HALVES], piece % HALVES
+            if half == 0:
                 weight_operands[g, s] = (
                     weight_pool.tile([P, HALVES, K_PASS], U32, name="w_codes_" + s, align_bytes=64),
                     weight_pool.tile([P, HALVES, K_PASS], U8, name="w_scales_" + s, align_bytes=64),
                 )
             w_codes, w_scales = weight_operands[g, s]
             nc.vector.quantize_mx(
-                out=w_codes[:, first:last, :].rearrange("p h w -> p (h w)").bitcast(FP8X4),
-                scales=w_scales[:, first:last, :].rearrange("p h w -> p (h w)"),
-                in_=grouped_weights[g, s][:, first:last, :, :].rearrange("p h w u -> p (h w u)"),
+                out=w_codes[:, half, :].bitcast(FP8X4),
+                scales=w_scales[:, half, :],
+                in_=grouped_pieces[m][:].rearrange("p w u -> p (w u)"),
             )
 
         def regroup_w2(q, copy, first, last):
@@ -332,9 +330,8 @@ def tile_stateencoder_pa_k_kernel(
                 regroup_piece(unit + LEAD + 1)
 
         def quantise_beside(unit):
-            g, piece = divmod(unit + LEAD, PIECES)
-            if unit + LEAD < ALL_PIECES and piece % HALVES == HALVES - 1:
-                quantise_weights(g, STREAMS[piece // HALVES], (0, HALVES))
+            if unit + LEAD < ALL_PIECES:
+                quantise_piece(unit + LEAD)
 
         acc = [acc_pool.tile([P, BANK], F32, name="acc%d" % blk) for blk in range(BLOCKS)]
         hidden_tiles = {}
@@ -445,15 +442,16 @@ def tile_stateencoder_pa_k_kernel(
         turn_tokens("utt")
         quantise_tokens("sp")
         repeat_side_i("sp", 0, 1)
-        quantise_weights(0, "sp", (0, 1))
+        quantise_piece(0)
         regroup_piece(1)
         turn_biases()
         regroup_piece(2)
-        quantise_weights(0, "sp", (1, 2))
+        quantise_piece(1)
         quantise_tokens("utt")
         repeat_side_i("utt", 0, 1)
         regroup_piece(3)
-        quantise_weights(0, "utt", (0, HALVES))
+        quantise_piece(2)
+        quantise_piece(3)
         mix_weights()
         for s in STREAMS:
             repeat_side_i(s, 1, BLOCKS)
@@ -461,6 +459,7 @@ def tile_stateencoder_pa_k_kernel(
         regroup_piece(4)
         quantise_w2(0)
         regroup_piece(5)
+        quantise_piece(4)
 
         for unit in range(UNITS + LAG):
             if unit < UNITS:

@@ -34,9 +34,8 @@ PIECES = len(STREAMS) * HALVES
 ALL_PIECES = GROUPS * PIECES
 LAG = 2
 LEAD = PIECES + 1
-SCALAR_COLUMNS = 192
-SCALAR_PIECES = (0, 2)
-VECTOR_PIECES = (1, 3, 4, 5)
+SCALAR_COLUMNS = 160
+SCALAR_PARTS = len(STREAMS)
 MAX_LOGIT_GAP = 40.0
 
 FLOPS = 4 * 2 * TOKENS * D * H + 2 * PAIRS * H * OUT
@@ -259,29 +258,31 @@ def tile_stateencoder_pa_k_kernel(
         grouped_w2 = {}
         weight_operands = {}
 
-        def regroup_piece(m):
+        def start_piece(m):
             g, piece = divmod(m, PIECES)
             s, half = STREAMS[piece // HALVES], piece % HALVES
             half_rows = slice(half * PACK, (half + 1) * PACK)
             grouped = grouped_pool.tile([P, K_PASS, PACK], BF16, name="grouped", align_bytes=64)
             grouped_pieces[m] = grouped
-            if m in SCALAR_PIECES:
-                split = 0
-            elif m in VECTOR_PIECES:
-                split = K_PASS
-            else:
-                split = K_PASS - SCALAR_COLUMNS
-            for copy, share in (
-                (nc.vector.tensor_copy, slice(0, split)),
-                (nc.scalar.copy, slice(split, K_PASS)),
-            ):
-                if share.start < share.stop:
-                    copy(
-                        out=grouped[:, share, :].rearrange("p (c i) u -> p c u i", i=RUN),
-                        in_=raw_groups[g, s][:, half_rows, share].rearrange(
-                            "p u (c i) -> p c u i", i=RUN
-                        ),
-                    )
+
+            def regroup(copy, first, last):
+                share = slice(first, last)
+                copy(
+                    out=grouped[:, share, :].rearrange("p (c i) u -> p c u i", i=RUN),
+                    in_=raw_groups[g, s][:, half_rows, share].rearrange(
+                        "p u (c i) -> p c u i", i=RUN
+                    ),
+                )
+
+            return regroup
+
+        def regroup_whole(m, copy):
+            start_piece(m)(copy, 0, K_PASS)
+            end_piece(m)
+
+        def end_piece(m):
+            g, piece = divmod(m, PIECES)
+            s, half = STREAMS[piece // HALVES], piece % HALVES
             if half == HALVES - 1 and g + 2 < GROUPS:
                 load_weights(g + 2, s, 1)
 
@@ -325,10 +326,6 @@ def tile_stateencoder_pa_k_kernel(
             for i in range(W2_SET):
                 weight_operands[q * W2_SET + i, "W2"] = (w2_codes[:, i, :], w2_scales[:, i, :])
 
-        def regroup_beside(unit):
-            if unit + LEAD + 1 < ALL_PIECES:
-                regroup_piece(unit + LEAD + 1)
-
         def quantise_beside(unit):
             if unit + LEAD < ALL_PIECES:
                 quantise_piece(unit + LEAD)
@@ -338,7 +335,7 @@ def tile_stateencoder_pa_k_kernel(
         state_tiles = {}
         state_operands = {}
 
-        def first_stage(unit):
+        def first_stage(unit, scalar_work):
             g, blk = divmod(unit, BLOCKS)
             side_range = {"j": slice(0, BANK), "i": slice(blk * BANK, (blk + 1) * BANK)}
             for s in STREAMS:
@@ -366,6 +363,8 @@ def tile_stateencoder_pa_k_kernel(
                         scale=1.0,
                     )
                 hidden_tiles[unit, s] = hidden
+                for work in scalar_work[s]:
+                    work()
 
         def mix_streams(unit):
             hidden_utt = hidden_tiles[unit, "utt"]
@@ -438,39 +437,55 @@ def tile_stateencoder_pa_k_kernel(
                 finish_block(blk)
 
         turn_tokens("sp")
-        regroup_piece(0)
+        regroup_whole(0, nc.scalar.copy)
         turn_tokens("utt")
         quantise_tokens("sp")
         repeat_side_i("sp", 0, 1)
         quantise_piece(0)
-        regroup_piece(1)
+        regroup_whole(1, nc.vector.tensor_copy)
         turn_biases()
-        regroup_piece(2)
+        regroup_whole(2, nc.scalar.copy)
         quantise_piece(1)
         quantise_tokens("utt")
         repeat_side_i("utt", 0, 1)
-        regroup_piece(3)
+        regroup_whole(3, nc.vector.tensor_copy)
         quantise_piece(2)
         quantise_piece(3)
         mix_weights()
         for s in STREAMS:
             repeat_side_i(s, 1, BLOCKS)
         regroup_w2(0, nc.vector.tensor_copy, 0, W2_SET)
-        regroup_piece(4)
+        regroup_whole(4, nc.vector.tensor_copy)
         quantise_w2(0)
-        regroup_piece(5)
+        regroup_whole(5, nc.vector.tensor_copy)
         quantise_piece(4)
 
         for unit in range(UNITS + LAG):
             if unit < UNITS:
-                first_stage(unit)
                 q, step = divmod(unit, SET_UNITS)
                 i, blk = divmod(step, BLOCKS)
                 more_w2 = (q + 1) * W2_SET < GROUPS
+                scalar_work = {s: [] for s in STREAMS}
                 if more_w2 and blk == 1:
-                    regroup_w2(q + 1, nc.scalar.copy, i, i + 1)
+                    scalar_work["sp"].append(
+                        lambda q=q, i=i: regroup_w2(q + 1, nc.scalar.copy, i, i + 1)
+                    )
+                m = unit + LEAD + 1
+                regroup = start_piece(m) if m < ALL_PIECES else None
+                if regroup:
+                    part = SCALAR_COLUMNS // SCALAR_PARTS
+                    for k, s in enumerate(STREAMS):
+                        first = K_PASS - SCALAR_COLUMNS + k * part
+                        scalar_work[s].append(
+                            lambda regroup=regroup, first=first: regroup(
+                                nc.scalar.copy, first, first + part
+                            )
+                        )
+                first_stage(unit, scalar_work)
                 mix_streams(unit)
-                regroup_beside(unit)
+                if regroup:
+                    regroup(nc.vector.tensor_copy, 0, K_PASS - SCALAR_COLUMNS)
+                    end_piece(m)
                 round_state(unit)
                 quantise_beside(unit)
                 if more_w2 and step == SET_UNITS - 2:

@@ -30,12 +30,10 @@ SET_UNITS = W2_SET * BLOCKS
 STREAMS = ("sp", "utt")
 SIDES = ("j", "i")
 HALVES = len(SIDES)
-PIECES = len(STREAMS) * HALVES
-ALL_PIECES = GROUPS * PIECES
-LAG = 2
-LEAD = PIECES + 1
+ALL_PAIRS = GROUPS * len(STREAMS)
+LAG = 3
+LEAD = 3
 SCALAR_COLUMNS = 160
-SCALAR_PARTS = len(STREAMS)
 MAX_LOGIT_GAP = 40.0
 
 FLOPS = 4 * 2 * TOKENS * D * H + 2 * PAIRS * H * OUT
@@ -52,9 +50,9 @@ def tile_stateencoder_pa_k_kernel(
     with ExitStack() as ctx:
         ctx.enter_context(tc.manual_schedule())
         const = ctx.enter_context(tc.tile_pool(name="const", bufs=1))
-        stage = ctx.enter_context(tc.tile_pool(name="stage", bufs=2))
+        stage = ctx.enter_context(tc.tile_pool(name="stage", bufs=1))
         raw_pool = ctx.enter_context(tc.tile_pool(name="raw", bufs=4))
-        grouped_pool = ctx.enter_context(tc.tile_pool(name="grouped", bufs=3))
+        grouped_pool = ctx.enter_context(tc.tile_pool(name="grouped", bufs=2))
         weight_pool = ctx.enter_context(tc.tile_pool(name="weights", bufs=3))
         hidden_pool = ctx.enter_context(tc.tile_pool(name="hidden", bufs=LAG + 1))
         state_pool = ctx.enter_context(tc.tile_pool(name="state", bufs=LAG + 2))
@@ -254,51 +252,44 @@ def tile_stateencoder_pa_k_kernel(
             nc.vector.reciprocal(out=weight_sp[:], in_=denominator[:])
             nc.gpsimd.tensor_mul(out=gain_sp[:], in0=weight_sp[:], in1=gain[:])
 
-        grouped_pieces = {}
+        grouped_pairs = {}
         grouped_w2 = {}
         weight_operands = {}
 
-        def start_piece(m):
-            g, piece = divmod(m, PIECES)
-            s, half = STREAMS[piece // HALVES], piece % HALVES
-            half_rows = slice(half * PACK, (half + 1) * PACK)
-            grouped = grouped_pool.tile([P, K_PASS, PACK], BF16, name="grouped", align_bytes=64)
-            grouped_pieces[m] = grouped
-
-            def regroup(copy, first, last):
-                share = slice(first, last)
-                copy(
-                    out=grouped[:, share, :].rearrange("p (c i) u -> p c u i", i=RUN),
-                    in_=raw_groups[g, s][:, half_rows, share].rearrange(
-                        "p u (c i) -> p c u i", i=RUN
-                    ),
+        def regroup(n, copy, halves, columns):
+            g, k = divmod(n, len(STREAMS))
+            rows = slice(halves.start * PACK, halves.stop * PACK)
+            if n not in grouped_pairs:
+                grouped_pairs[n] = grouped_pool.tile(
+                    [P, HALVES, K_PASS, PACK], BF16, name="grouped", align_bytes=64
                 )
+            copy(
+                out=grouped_pairs[n][:, halves, columns, :].rearrange(
+                    "p h (c i) u -> p h c u i", i=RUN
+                ),
+                in_=raw_groups[g, STREAMS[k]][:, rows, columns].rearrange(
+                    "p (h u) (c i) -> p h c u i", u=PACK, i=RUN
+                ),
+            )
 
-            return regroup
+        def load_again(n):
+            g, k = divmod(n, len(STREAMS))
+            if g + 2 < GROUPS:
+                load_weights(g + 2, STREAMS[k], 1)
 
-        def regroup_whole(m, copy):
-            start_piece(m)(copy, 0, K_PASS)
-            end_piece(m)
-
-        def end_piece(m):
-            g, piece = divmod(m, PIECES)
-            s, half = STREAMS[piece // HALVES], piece % HALVES
-            if half == HALVES - 1 and g + 2 < GROUPS:
-                load_weights(g + 2, s, 1)
-
-        def quantise_piece(m):
-            g, piece = divmod(m, PIECES)
-            s, half = STREAMS[piece // HALVES], piece % HALVES
-            if half == 0:
+        def quantise_pair(n, halves):
+            g, k = divmod(n, len(STREAMS))
+            s = STREAMS[k]
+            if halves.start == 0:
                 weight_operands[g, s] = (
                     weight_pool.tile([P, HALVES, K_PASS], U32, name="w_codes_" + s, align_bytes=64),
                     weight_pool.tile([P, HALVES, K_PASS], U8, name="w_scales_" + s, align_bytes=64),
                 )
             w_codes, w_scales = weight_operands[g, s]
             nc.vector.quantize_mx(
-                out=w_codes[:, half, :].bitcast(FP8X4),
-                scales=w_scales[:, half, :],
-                in_=grouped_pieces[m][:].rearrange("p w u -> p (w u)"),
+                out=w_codes[:, halves, :].rearrange("p h w -> p (h w)").bitcast(FP8X4),
+                scales=w_scales[:, halves, :].rearrange("p h w -> p (h w)"),
+                in_=grouped_pairs[n][:, halves, :, :].rearrange("p h w u -> p (h w u)"),
             )
 
         def regroup_w2(q, copy, first, last):
@@ -325,10 +316,6 @@ def tile_stateencoder_pa_k_kernel(
             )
             for i in range(W2_SET):
                 weight_operands[q * W2_SET + i, "W2"] = (w2_codes[:, i, :], w2_scales[:, i, :])
-
-        def quantise_beside(unit):
-            if unit + LEAD < ALL_PIECES:
-                quantise_piece(unit + LEAD)
 
         acc = [acc_pool.tile([P, BANK], F32, name="acc%d" % blk) for blk in range(BLOCKS)]
         hidden_tiles = {}
@@ -436,60 +423,69 @@ def tile_stateencoder_pa_k_kernel(
             if g == GROUPS - 1:
                 finish_block(blk)
 
+        half_j, half_i, both = slice(0, 1), slice(1, 2), slice(0, HALVES)
+        all_columns = slice(0, K_PASS)
+        vector_columns = slice(0, K_PASS - SCALAR_COLUMNS)
+        scalar_columns = slice(K_PASS - SCALAR_COLUMNS, K_PASS)
         turn_tokens("sp")
-        regroup_whole(0, nc.scalar.copy)
+        regroup(0, nc.scalar.copy, half_j, all_columns)
         turn_tokens("utt")
         quantise_tokens("sp")
         repeat_side_i("sp", 0, 1)
-        quantise_piece(0)
-        regroup_whole(1, nc.vector.tensor_copy)
+        quantise_pair(0, half_j)
+        regroup(0, nc.vector.tensor_copy, half_i, all_columns)
+        load_again(0)
         turn_biases()
-        regroup_whole(2, nc.scalar.copy)
-        quantise_piece(1)
+        regroup(1, nc.scalar.copy, half_j, all_columns)
+        quantise_pair(0, half_i)
         quantise_tokens("utt")
         repeat_side_i("utt", 0, 1)
-        regroup_whole(3, nc.vector.tensor_copy)
-        quantise_piece(2)
-        quantise_piece(3)
+        regroup(1, nc.vector.tensor_copy, half_i, all_columns)
+        load_again(1)
         mix_weights()
+        quantise_pair(1, both)
         for s in STREAMS:
             repeat_side_i(s, 1, BLOCKS)
         regroup_w2(0, nc.vector.tensor_copy, 0, W2_SET)
-        regroup_whole(4, nc.vector.tensor_copy)
+        regroup(2, nc.vector.tensor_copy, both, all_columns)
+        load_again(2)
         quantise_w2(0)
-        regroup_whole(5, nc.vector.tensor_copy)
-        quantise_piece(4)
+        quantise_pair(2, both)
 
         for unit in range(UNITS + LAG):
             if unit < UNITS:
+                n, odd = divmod(unit, 2)
+                n += LEAD
                 q, step = divmod(unit, SET_UNITS)
                 i, blk = divmod(step, BLOCKS)
                 more_w2 = (q + 1) * W2_SET < GROUPS
                 scalar_work = {s: [] for s in STREAMS}
-                if more_w2 and blk == 1:
+                if n < ALL_PAIRS:
                     scalar_work["sp"].append(
+                        lambda n=n, half=(half_i if odd else half_j): regroup(
+                            n, nc.scalar.copy, half, scalar_columns
+                        )
+                    )
+                if more_w2 and blk == 1:
+                    scalar_work["utt"].append(
                         lambda q=q, i=i: regroup_w2(q + 1, nc.scalar.copy, i, i + 1)
                     )
-                m = unit + LEAD + 1
-                regroup = start_piece(m) if m < ALL_PIECES else None
-                if regroup:
-                    part = SCALAR_COLUMNS // SCALAR_PARTS
-                    for k, s in enumerate(STREAMS):
-                        first = K_PASS - SCALAR_COLUMNS + k * part
-                        scalar_work[s].append(
-                            lambda regroup=regroup, first=first: regroup(
-                                nc.scalar.copy, first, first + part
-                            )
-                        )
                 first_stage(unit, scalar_work)
+                last = unit == UNITS - 1
+                if last:
+                    quantise_state(unit - 1)
                 mix_streams(unit)
-                if regroup:
-                    regroup(nc.vector.tensor_copy, 0, K_PASS - SCALAR_COLUMNS)
-                    end_piece(m)
+                if unit > 0 and not last:
+                    quantise_state(unit - 1)
+                if n < ALL_PAIRS and odd:
+                    load_again(n)
+                    quantise_pair(n, both)
+                elif n < ALL_PAIRS:
+                    regroup(n, nc.vector.tensor_copy, both, vector_columns)
                 round_state(unit)
-                quantise_beside(unit)
                 if more_w2 and step == SET_UNITS - 2:
                     quantise_w2(q + 1)
-                quantise_state(unit)
+                if last:
+                    quantise_state(unit)
             if unit >= LAG:
                 second_stage(unit - LAG)

@@ -17,21 +17,23 @@ PACK = 4
 K_PASS = P * PACK
 WORD = 4
 RUN = 4
+SCALAR_RUN = 8
 B, L, D, H, OUT = 8, 16, 512, 8192, 128
 TOKENS = B * L
 PAIRS = B * L * L
 BANK = 512
 BLOCKS = PAIRS // BANK
-ROWS = L // BLOCKS
 GROUPS = H // K_PASS
 UNITS = GROUPS * BLOCKS
+TWIN = 2
 W2_SET = 4
 SET_UNITS = W2_SET * BLOCKS
 STREAMS = ("sp", "utt")
 SIDES = ("j", "i")
 HALVES = len(SIDES)
 ALL_PAIRS = GROUPS * len(STREAMS)
-LAG = 3
+LAG = 5
+AHEAD = 3
 LEAD = 3
 SCALAR_COLUMNS = 160
 MAX_LOGIT_GAP = 40.0
@@ -54,9 +56,9 @@ def tile_stateencoder_pa_k_kernel(
         raw_pool = ctx.enter_context(tc.tile_pool(name="raw", bufs=4))
         grouped_pool = ctx.enter_context(tc.tile_pool(name="grouped", bufs=2))
         weight_pool = ctx.enter_context(tc.tile_pool(name="weights", bufs=3))
-        hidden_pool = ctx.enter_context(tc.tile_pool(name="hidden", bufs=LAG + 1))
-        state_pool = ctx.enter_context(tc.tile_pool(name="state", bufs=LAG + 2))
-        result_pool = ctx.enter_context(tc.tile_pool(name="result", bufs=2))
+        hidden_pool = ctx.enter_context(tc.tile_pool(name="hidden", bufs=AHEAD + 1))
+        state_pool = ctx.enter_context(tc.tile_pool(name="state", bufs=2))
+        result_pool = ctx.enter_context(tc.tile_pool(name="result", bufs=3))
         acc_pool = ctx.enter_context(tc.psum_pool(name="acc", bufs=1))
         bank_pool = ctx.enter_context(tc.psum_pool(name="bank", bufs=4))
 
@@ -142,41 +144,27 @@ def tile_stateencoder_pa_k_kernel(
 
         pair_codes = {}
         pair_scales = {}
-        side_columns = {"j": BANK, "i": PAIRS}
         token_planes = {}
         for s in STREAMS:
-            for side in SIDES:
+            for side, columns in (("i", BANK), ("j", PAIRS)):
                 pair_codes[s, side] = const.tile(
-                    [P, side_columns[side]],
-                    U32,
-                    name="pair_codes_%s_%s" % (s, side),
-                    align_bytes=64,
+                    [P, columns], U32, name="pair_codes_%s_%s" % (s, side), align_bytes=64
                 )
                 pair_scales[s, side] = const.tile(
-                    [P, side_columns[side]],
-                    U8,
-                    name="pair_scales_%s_%s" % (s, side),
-                    align_bytes=64,
+                    [P, columns], U8, name="pair_scales_%s_%s" % (s, side), align_bytes=64
                 )
+            token_codes = const.tile([P, TOKENS], U32, name="token_codes_" + s, align_bytes=64)
             token_scales = const.tile([P, TOKENS], U8, name="token_scales_" + s, align_bytes=64)
             nc.gpsimd.memset(token_scales[:].bitcast(I32), 0)
-            fourfold_scales = const.tile(
-                [P, TOKENS * WORD], U8, name="fourfold_scales_" + s, align_bytes=64
-            )
-            nc.gpsimd.memset(fourfold_scales[:].bitcast(I32), 0)
-            token_codes = const.tile([P, TOKENS], U32, name="token_codes_" + s, align_bytes=64)
-            token_planes[s] = (token_codes, token_scales, fourfold_scales)
+            token_planes[s] = (token_codes, token_scales)
 
         ident_f32 = const.tile([P, P], F32, name="ident_f32")
         masks.make_identity(nc, ident_f32[:])
 
         def quantise_tokens(s):
             grouped = token_grouped[s]
-            token_codes, token_scales, fourfold_scales = token_planes[s]
+            token_codes, token_scales = token_planes[s]
             fourfold = stage.tile([P, TOKENS, WORD, PACK], BF16, name="fourfold", align_bytes=64)
-            fourfold_codes = stage.tile(
-                [P, TOKENS * WORD], U32, name="fourfold_codes", align_bytes=64
-            )
             nc.vector.tensor_copy(
                 out=fourfold[:], in_=grouped[:].unsqueeze(2).to_broadcast([P, TOKENS, WORD, PACK])
             )
@@ -186,47 +174,35 @@ def tile_stateencoder_pa_k_kernel(
                 in_=grouped[:].rearrange("p r u -> p (r u)"),
             )
             nc.vector.quantize_mx(
-                out=fourfold_codes[:].bitcast(FP8X4),
-                scales=fourfold_scales[:],
+                out=pair_codes[s, "i"][:].bitcast(FP8X4),
+                scales=pair_scales[s, "i"][:],
                 in_=fourfold[:].rearrange("p r f u -> p (r f u)"),
             )
+
+        def repeat_side_j(s, first, last):
+            token_codes, token_scales = token_planes[s]
+            columns = slice(first * BANK, last * BANK)
+            blocks = last - first
             nc.vector.tensor_copy(
-                out=pair_codes[s, "j"][:]
+                out=pair_codes[s, "j"][:, columns]
                 .bitcast(I32)
-                .rearrange("p (b i j) -> p b i j", b=B, i=ROWS),
+                .rearrange("p (k b i j) -> p b k i j", k=blocks, b=B, j=WORD),
                 in_=token_codes[:]
                 .bitcast(I32)
-                .rearrange("p (b j) -> p b j", b=B)
-                .unsqueeze(2)
-                .to_broadcast([P, B, ROWS, L]),
+                .rearrange("p (b k j) -> p b k j", b=B, j=WORD)[:, :, first:last, :]
+                .unsqueeze(3)
+                .to_broadcast([P, B, blocks, L, WORD]),
             )
             nc.vector.tensor_copy(
-                out=pair_scales[s, "j"][:]
+                out=pair_scales[s, "j"][:, columns]
                 .bitcast(I32)
-                .rearrange("p (b i w) -> p b i w", b=B, i=ROWS),
+                .rearrange("p (k b i) -> p b k i", k=blocks, b=B),
                 in_=token_scales[:]
                 .bitcast(I32)
-                .rearrange("p (b w) -> p b w", b=B)
-                .unsqueeze(2)
-                .to_broadcast([P, B, ROWS, L // WORD]),
+                .rearrange("p (b k) -> p b k", b=B)[:, :, first:last]
+                .unsqueeze(3)
+                .to_broadcast([P, B, blocks, L]),
             )
-
-        def repeat_side_i(s, first, last):
-            token_codes, token_scales, fourfold_scales = token_planes[s]
-            for plane, repeated, words in (
-                (token_codes, pair_codes[s, "i"], L),
-                (fourfold_scales, pair_scales[s, "i"], L // WORD),
-            ):
-                nc.vector.tensor_copy(
-                    out=repeated[:, first * BANK : last * BANK]
-                    .bitcast(I32)
-                    .rearrange("p (k b i w) -> p b k i w", k=last - first, b=B, i=ROWS),
-                    in_=plane[:]
-                    .bitcast(I32)
-                    .rearrange("p (b k i) -> p b k i", b=B, i=ROWS)[:, :, first:last, :]
-                    .unsqueeze(4)
-                    .to_broadcast([P, B, last - first, ROWS, words]),
-                )
 
         mix = const.tile([P, 2], F32, name="mix")
         gain = const.tile([P, 1], F32, name="gain")
@@ -252,11 +228,15 @@ def tile_stateencoder_pa_k_kernel(
             nc.vector.reciprocal(out=weight_sp[:], in_=denominator[:])
             nc.gpsimd.tensor_mul(out=gain_sp[:], in0=weight_sp[:], in1=gain[:])
 
+        half_j, half_i, both = slice(0, 1), slice(1, 2), slice(0, HALVES)
+        all_columns = slice(0, K_PASS)
+        vector_columns = slice(0, K_PASS - SCALAR_COLUMNS)
+        scalar_columns = slice(K_PASS - SCALAR_COLUMNS, K_PASS)
         grouped_pairs = {}
         grouped_w2 = {}
         weight_operands = {}
 
-        def regroup(n, copy, halves, columns):
+        def regroup(n, copy, run, halves, columns):
             g, k = divmod(n, len(STREAMS))
             rows = slice(halves.start * PACK, halves.stop * PACK)
             if n not in grouped_pairs:
@@ -265,10 +245,10 @@ def tile_stateencoder_pa_k_kernel(
                 )
             copy(
                 out=grouped_pairs[n][:, halves, columns, :].rearrange(
-                    "p h (c i) u -> p h c u i", i=RUN
+                    "p h (c i) u -> p h c u i", i=run
                 ),
                 in_=raw_groups[g, STREAMS[k]][:, rows, columns].rearrange(
-                    "p (h u) (c i) -> p h c u i", u=PACK, i=RUN
+                    "p (h u) (c i) -> p h c u i", u=PACK, i=run
                 ),
             )
 
@@ -292,15 +272,15 @@ def tile_stateencoder_pa_k_kernel(
                 in_=grouped_pairs[n][:, halves, :, :].rearrange("p h w u -> p (h w u)"),
             )
 
-        def regroup_w2(q, copy, first, last):
+        def regroup_w2(q, copy, run, first, last):
             if first == 0:
                 grouped_w2[q] = grouped_pool.tile(
                     [P, W2_SET, OUT, PACK], BF16, name="grouped_w2", bufs=1, align_bytes=64
                 )
             copy(
-                out=grouped_w2[q][:, first:last, :, :],
+                out=grouped_w2[q][:, first:last, :, :].rearrange("p g (c i) t -> p g c t i", i=run),
                 in_=raw_groups[q, "W2"][:, first * PACK : last * PACK, :].rearrange(
-                    "p (g t) o -> p g o t", t=PACK
+                    "p (g t) (c i) -> p g c t i", t=PACK, i=run
                 ),
             )
             if last == W2_SET and (q + 1) * W2_SET < GROUPS:
@@ -320,11 +300,11 @@ def tile_stateencoder_pa_k_kernel(
         acc = [acc_pool.tile([P, BANK], F32, name="acc%d" % blk) for blk in range(BLOCKS)]
         hidden_tiles = {}
         state_tiles = {}
-        state_operands = {}
+        state_words = {}
 
         def first_stage(unit, scalar_work):
             g, blk = divmod(unit, BLOCKS)
-            side_range = {"j": slice(0, BANK), "i": slice(blk * BANK, (blk + 1) * BANK)}
+            side_range = {"i": slice(0, BANK), "j": slice(blk * BANK, (blk + 1) * BANK)}
             for s in STREAMS:
                 w_codes, w_scales = weight_operands[g, s]
                 hidden = hidden_pool.tile([P, PACK, BANK], F32, name="hidden_" + s)
@@ -367,94 +347,105 @@ def tile_stateencoder_pa_k_kernel(
                     op1=ALU.add,
                 )
 
-        def round_state(unit):
-            state = state_pool.tile([P, BANK, PACK], BF16, name="state", bufs=2, align_bytes=64)
-            nc.vector.tensor_scalar(
-                out=state[:].rearrange("p (c i) t -> p c t i", i=RUN),
-                in0=hidden_tiles[unit, "utt"][:].rearrange("p t (c i) -> p c t i", i=RUN),
-                scalar1=gain_sp[:, 0:1],
-                scalar2=None,
-                op0=ALU.mult,
+        def round_state(unit, engine, columns):
+            twin, k = divmod(unit, TWIN)
+            if twin not in state_tiles:
+                state_tiles[twin] = state_pool.tile(
+                    [P, TWIN, BANK, PACK], BF16, name="state", align_bytes=64
+                )
+            packed = state_tiles[twin][:, k, columns, :].rearrange("p (c i) t -> p c t i", i=RUN)
+            mixed = hidden_tiles[unit, "utt"][:, :, columns].rearrange(
+                "p t (c i) -> p c t i", i=RUN
             )
-            state_tiles[unit] = state
+            if engine == "vector":
+                nc.vector.tensor_scalar(
+                    out=packed, in0=mixed, scalar1=gain_sp[:, 0:1], scalar2=None, op0=ALU.mult
+                )
+            else:
+                nc.scalar.activation(out=packed, in_=mixed, func=ACT.Copy, scale=gain_sp[:, 0:1])
 
-        def quantise_state(unit):
-            state_codes = state_pool.tile([P, BANK], U32, name="state_codes", align_bytes=64)
-            state_scales = state_pool.tile([P, BANK], U8, name="state_scales", align_bytes=64)
+        def quantise_states(twin, first, last):
+            if first == 0:
+                state_words[twin] = (
+                    state_pool.tile([P, TWIN, BANK], U32, name="state_codes", bufs=3, align_bytes=64),
+                    state_pool.tile([P, TWIN, BANK], U8, name="state_scales", bufs=3, align_bytes=64),
+                )
+            state_codes, state_scales = state_words[twin]
             nc.vector.quantize_mx(
-                out=state_codes[:].bitcast(FP8X4),
-                scales=state_scales[:],
-                in_=state_tiles[unit][:].rearrange("p c t -> p (c t)"),
+                out=state_codes[:, first:last, :].rearrange("p k c -> p (k c)").bitcast(FP8X4),
+                scales=state_scales[:, first:last, :].rearrange("p k c -> p (k c)"),
+                in_=state_tiles[twin][:, first:last, :, :].rearrange("p k c t -> p (k c t)"),
             )
-            state_operands[unit] = (state_codes, state_scales)
 
-        PAIR = P // (ROWS * L)
-        out_rows = out.rearrange("(r h) (k i) j o -> k h i j r o", h=PAIR, k=BLOCKS)
+        out_rows = out.rearrange("b i (k j) o -> k (b i) j o", j=WORD)
 
         def finish_block(blk):
-            result = result_pool.tile([P, BANK], F32, name="result")
-            nc.scalar.activation(
-                out=result[:], in_=acc[blk][:], func=ACT.Tanh, bias=b2_col[:, 0:1], scale=1.0
-            )
-            turned = bank_pool.tile([P, BANK // P, OUT], F32, name="turned", tag="bank")
-            for r in range(BANK // P):
-                nc.tensor.transpose(turned[:, r, :], result[:, r * P : (r + 1) * P], ident_f32[:])
-            result_rows = result_pool.tile([P, BANK // P, OUT], F32, name="result_rows")
-            nc.scalar.copy(out=result_rows[:], in_=turned[:])
-            for h, dma_start in enumerate((nc.sync.dma_start, nc.scalar.dma_start)):
-                dma_start(
-                    out=out_rows[blk, h].rearrange("i j r o -> (i j) r o"),
-                    in_=result_rows[h * ROWS * L : (h + 1) * ROWS * L, :, :],
+            last = blk == BLOCKS - 1
+            step = WORD // 2 if last else WORD
+            for first in range(0, WORD, step):
+                result = result_pool.tile([P, step, TOKENS], F32, name="result")
+                nc.scalar.activation(
+                    out=result[:],
+                    in_=acc[blk][:].rearrange("p (r j) -> p j r", j=WORD)[:, first : first + step, :],
+                    func=ACT.Tanh,
+                    bias=b2_col[:, 0:1],
+                    scale=1.0,
+                )
+                turned = bank_pool.tile([P, step, OUT], F32, name="turned", tag="bank")
+                for j in range(step):
+                    nc.tensor.transpose(turned[:, j, :], result[:, j, :], ident_f32[:])
+                result_rows = result_pool.tile([P, step, OUT], F32, name="result_rows")
+                copy = nc.vector.tensor_copy if last and first == 0 else nc.scalar.copy
+                copy(out=result_rows[:], in_=turned[:])
+                nc.sync.dma_start(
+                    out=out_rows[blk][:, first : first + step, :], in_=result_rows[:]
                 )
 
         def second_stage(unit):
             g, blk = divmod(unit, BLOCKS)
             w2_codes, w2_scales = weight_operands[g, "W2"]
-            state_codes, state_scales = state_operands[unit]
+            twin, k = divmod(unit, TWIN)
+            state_codes, state_scales = state_words[twin]
             nc.tensor.matmul_mx(
                 out=acc[blk][:],
                 lhsT=w2_codes.bitcast(FP8X4),
                 lhsT_scale=w2_scales,
-                rhs=state_codes[:].bitcast(FP8X4),
-                rhs_scale=state_scales[:],
+                rhs=state_codes[:, k, :].bitcast(FP8X4),
+                rhs_scale=state_scales[:, k, :],
                 start=(g == 0),
                 stop=(g == GROUPS - 1),
             )
             if g == GROUPS - 1:
                 finish_block(blk)
 
-        half_j, half_i, both = slice(0, 1), slice(1, 2), slice(0, HALVES)
-        all_columns = slice(0, K_PASS)
-        vector_columns = slice(0, K_PASS - SCALAR_COLUMNS)
-        scalar_columns = slice(K_PASS - SCALAR_COLUMNS, K_PASS)
         turn_tokens("sp")
-        regroup(0, nc.scalar.copy, half_j, all_columns)
+        regroup(0, nc.scalar.copy, SCALAR_RUN, half_j, all_columns)
         turn_tokens("utt")
         quantise_tokens("sp")
-        repeat_side_i("sp", 0, 1)
+        repeat_side_j("sp", 0, 1)
         quantise_pair(0, half_j)
-        regroup(0, nc.vector.tensor_copy, half_i, all_columns)
+        regroup(0, nc.vector.tensor_copy, RUN, half_i, all_columns)
         load_again(0)
         turn_biases()
-        regroup(1, nc.scalar.copy, half_j, all_columns)
+        regroup(1, nc.scalar.copy, SCALAR_RUN, half_j, all_columns)
         quantise_pair(0, half_i)
         quantise_tokens("utt")
-        repeat_side_i("utt", 0, 1)
-        regroup(1, nc.vector.tensor_copy, half_i, all_columns)
+        repeat_side_j("utt", 0, 1)
+        regroup(1, nc.vector.tensor_copy, RUN, half_i, all_columns)
         load_again(1)
         mix_weights()
         quantise_pair(1, both)
         for s in STREAMS:
-            repeat_side_i(s, 1, BLOCKS)
-        regroup_w2(0, nc.vector.tensor_copy, 0, W2_SET)
-        regroup(2, nc.vector.tensor_copy, both, all_columns)
+            repeat_side_j(s, 1, BLOCKS)
+        regroup_w2(0, nc.vector.tensor_copy, RUN, 0, W2_SET)
+        regroup(2, nc.vector.tensor_copy, RUN, both, all_columns)
         load_again(2)
         quantise_w2(0)
         quantise_pair(2, both)
 
         for unit in range(UNITS + LAG):
             if unit < UNITS:
-                n, odd = divmod(unit, 2)
+                n, odd = divmod(unit, TWIN)
                 n += LEAD
                 q, step = divmod(unit, SET_UNITS)
                 i, blk = divmod(step, BLOCKS)
@@ -463,29 +454,32 @@ def tile_stateencoder_pa_k_kernel(
                 if n < ALL_PAIRS:
                     scalar_work["sp"].append(
                         lambda n=n, half=(half_i if odd else half_j): regroup(
-                            n, nc.scalar.copy, half, scalar_columns
+                            n, nc.scalar.copy, SCALAR_RUN, half, scalar_columns
                         )
                     )
                 if more_w2 and blk == 1:
                     scalar_work["utt"].append(
-                        lambda q=q, i=i: regroup_w2(q + 1, nc.scalar.copy, i, i + 1)
+                        lambda q=q, i=i: regroup_w2(q + 1, nc.scalar.copy, SCALAR_RUN, i, i + 1)
                     )
                 first_stage(unit, scalar_work)
-                last = unit == UNITS - 1
-                if last:
-                    quantise_state(unit - 1)
+                if unit == UNITS - 1:
+                    round_state(unit - 1, "scalar", all_columns)
                 mix_streams(unit)
-                if unit > 0 and not last:
-                    quantise_state(unit - 1)
+                if unit > 0 and not odd:
+                    quantise_states(unit // TWIN - 1, 0, TWIN)
                 if n < ALL_PAIRS and odd:
                     load_again(n)
                     quantise_pair(n, both)
                 elif n < ALL_PAIRS:
-                    regroup(n, nc.vector.tensor_copy, both, vector_columns)
-                round_state(unit)
+                    regroup(n, nc.vector.tensor_copy, RUN, both, vector_columns)
+                if unit < UNITS - 2:
+                    round_state(unit, "vector", all_columns)
+                elif unit == UNITS - 1:
+                    round_state(unit, "vector", all_columns)
                 if more_w2 and step == SET_UNITS - 2:
                     quantise_w2(q + 1)
-                if last:
-                    quantise_state(unit)
+            if unit - LAG == UNITS - 2:
+                for k in range(TWIN):
+                    quantise_states(UNITS // TWIN - 1, k, k + 1)
             if unit >= LAG:
                 second_stage(unit - LAG)

@@ -35,7 +35,8 @@ ALL_PAIRS = GROUPS * len(STREAMS)
 LAG = 5
 AHEAD = 3
 LEAD = 3
-SCALAR_COLUMNS = 160
+SCALAR_COLUMNS = 104
+TENSOR_COLUMNS = 64
 MAX_LOGIT_GAP = 40.0
 
 FLOPS = 4 * 2 * TOKENS * D * H + 2 * PAIRS * H * OUT
@@ -230,27 +231,43 @@ def tile_stateencoder_pa_k_kernel(
 
         half_j, half_i, both = slice(0, 1), slice(1, 2), slice(0, HALVES)
         all_columns = slice(0, K_PASS)
-        vector_columns = slice(0, K_PASS - SCALAR_COLUMNS)
+        vector_columns = slice(0, K_PASS - SCALAR_COLUMNS - TENSOR_COLUMNS)
+        tensor_columns = slice(vector_columns.stop, vector_columns.stop + TENSOR_COLUMNS)
         scalar_columns = slice(K_PASS - SCALAR_COLUMNS, K_PASS)
         grouped_pairs = {}
         grouped_w2 = {}
         weight_operands = {}
 
-        def regroup(n, copy, run, halves, columns):
+        def grouped_and_raw(n, halves):
             g, k = divmod(n, len(STREAMS))
-            rows = slice(halves.start * PACK, halves.stop * PACK)
             if n not in grouped_pairs:
                 grouped_pairs[n] = grouped_pool.tile(
                     [P, HALVES, K_PASS, PACK], BF16, name="grouped", align_bytes=64
                 )
+            rows = slice(halves.start * PACK, halves.stop * PACK)
+            return grouped_pairs[n], raw_groups[g, STREAMS[k]][:, rows, :]
+
+        def regroup(n, copy, run, halves, columns):
+            grouped, raw = grouped_and_raw(n, halves)
             copy(
-                out=grouped_pairs[n][:, halves, columns, :].rearrange(
+                out=grouped[:, halves, columns, :].rearrange(
                     "p h (c i) u -> p h c u i", i=run
                 ),
-                in_=raw_groups[g, STREAMS[k]][:, rows, columns].rearrange(
-                    "p (h u) (c i) -> p h c u i", u=PACK, i=run
-                ),
+                in_=raw[:, :, columns].rearrange("p (h u) (c i) -> p h c u i", u=PACK, i=run),
             )
+
+        def regroup_by_tensor(n, halves, columns):
+            grouped, raw = grouped_and_raw(n, halves)
+            width = columns.stop - columns.start
+            packed = bank_pool.tile([P, width, PACK], BF16, name="packed", tag="bank")
+            nc.tensor.matmul(
+                out=packed[:],
+                lhsT=ident_bf[:],
+                rhs=raw[:, :, columns].rearrange("p u c -> p c u"),
+                start=True,
+                stop=True,
+            )
+            nc.scalar.copy(out=grouped[:, halves.start, columns, :], in_=packed[:])
 
         def load_again(n):
             g, k = divmod(n, len(STREAMS))
@@ -333,19 +350,16 @@ def tile_stateencoder_pa_k_kernel(
                 for work in scalar_work[s]:
                     work()
 
-        def mix_streams(unit):
+        def mix_streams(unit, chunks):
             hidden_utt = hidden_tiles[unit, "utt"]
-            step = 1 if unit == UNITS - 1 else PACK
-            for t in range(0, PACK, step):
-                chunks = slice(t, t + step)
-                nc.vector.scalar_tensor_tensor(
-                    out=hidden_utt[:, chunks, :],
-                    in0=hidden_utt[:, chunks, :],
-                    scalar=ratio[:, 0:1],
-                    in1=hidden_tiles[unit, "sp"][:, chunks, :],
-                    op0=ALU.mult,
-                    op1=ALU.add,
-                )
+            nc.vector.scalar_tensor_tensor(
+                out=hidden_utt[:, chunks, :],
+                in0=hidden_utt[:, chunks, :],
+                scalar=ratio[:, 0:1],
+                in1=hidden_tiles[unit, "sp"][:, chunks, :],
+                op0=ALU.mult,
+                op1=ALU.add,
+            )
 
         def round_state(unit, engine, columns):
             twin, k = divmod(unit, TWIN)
@@ -379,27 +393,39 @@ def tile_stateencoder_pa_k_kernel(
 
         out_rows = out.rearrange("b i (k j) o -> k (b i) j o", j=WORD)
 
-        def finish_block(blk):
-            last = blk == BLOCKS - 1
-            step = WORD // 2 if last else WORD
-            for first in range(0, WORD, step):
-                result = result_pool.tile([P, step, TOKENS], F32, name="result")
+        results = {}
+
+        def parts(blk):
+            step = WORD // 2 if blk == BLOCKS - 1 else WORD
+            return [slice(first, first + step) for first in range(0, WORD, step)]
+
+        def squash_block(blk):
+            columns = acc[blk][:].rearrange("p (r j) -> p j r", j=WORD)
+            for part in parts(blk):
+                result = result_pool.tile([P, part.stop - part.start, TOKENS], F32, name="result")
                 nc.scalar.activation(
                     out=result[:],
-                    in_=acc[blk][:].rearrange("p (r j) -> p j r", j=WORD)[:, first : first + step, :],
+                    in_=columns[:, part, :],
                     func=ACT.Tanh,
                     bias=b2_col[:, 0:1],
                     scale=1.0,
                 )
-                turned = bank_pool.tile([P, step, OUT], F32, name="turned", tag="bank")
-                for j in range(step):
-                    nc.tensor.transpose(turned[:, j, :], result[:, j, :], ident_f32[:])
-                result_rows = result_pool.tile([P, step, OUT], F32, name="result_rows")
-                copy = nc.vector.tensor_copy if last and first == 0 else nc.scalar.copy
-                copy(out=result_rows[:], in_=turned[:])
-                nc.sync.dma_start(
-                    out=out_rows[blk][:, first : first + step, :], in_=result_rows[:]
+                results[blk, part.start] = result
+
+        def store_block(blk):
+            for part in parts(blk):
+                result = results[blk, part.start]
+                turned = bank_pool.tile(
+                    [P, part.stop - part.start, OUT], F32, name="turned", tag="bank"
                 )
+                for j in range(part.stop - part.start):
+                    nc.tensor.transpose(turned[:, j, :], result[:, j, :], ident_f32[:])
+                result_rows = result_pool.tile(
+                    [P, part.stop - part.start, OUT], F32, name="result_rows"
+                )
+                copy = nc.vector.tensor_copy if part.stop < WORD else nc.scalar.copy
+                copy(out=result_rows[:], in_=turned[:])
+                nc.sync.dma_start(out=out_rows[blk][:, part, :], in_=result_rows[:])
 
         def second_stage(unit):
             g, blk = divmod(unit, BLOCKS)
@@ -416,7 +442,10 @@ def tile_stateencoder_pa_k_kernel(
                 stop=(g == GROUPS - 1),
             )
             if g == GROUPS - 1:
-                finish_block(blk)
+                squash_block(blk)
+                if blk > 0:
+                    for ready in (0, 1) if blk == 1 else (blk,):
+                        store_block(ready)
 
         turn_tokens("sp")
         regroup(0, nc.scalar.copy, SCALAR_RUN, half_j, all_columns)
@@ -452,8 +481,12 @@ def tile_stateencoder_pa_k_kernel(
                 more_w2 = (q + 1) * W2_SET < GROUPS
                 scalar_work = {s: [] for s in STREAMS}
                 if n < ALL_PAIRS:
+                    half = half_i if odd else half_j
                     scalar_work["sp"].append(
-                        lambda n=n, half=(half_i if odd else half_j): regroup(
+                        lambda n=n, half=half: regroup_by_tensor(n, half, tensor_columns)
+                    )
+                    scalar_work["sp"].append(
+                        lambda n=n, half=half: regroup(
                             n, nc.scalar.copy, SCALAR_RUN, half, scalar_columns
                         )
                     )
@@ -462,9 +495,14 @@ def tile_stateencoder_pa_k_kernel(
                         lambda q=q, i=i: regroup_w2(q + 1, nc.scalar.copy, SCALAR_RUN, i, i + 1)
                     )
                 first_stage(unit, scalar_work)
-                if unit == UNITS - 1:
+                if unit < UNITS - 1:
+                    mix_streams(unit, slice(0, PACK))
+                else:
                     round_state(unit - 1, "scalar", all_columns)
-                mix_streams(unit)
+                    for chunk in range(PACK):
+                        if chunk == PACK // 2:
+                            quantise_states(unit // TWIN, 0, 1)
+                        mix_streams(unit, slice(chunk, chunk + 1))
                 if unit > 0 and not odd:
                     quantise_states(unit // TWIN - 1, 0, TWIN)
                 if n < ALL_PAIRS and odd:
@@ -472,14 +510,11 @@ def tile_stateencoder_pa_k_kernel(
                     quantise_pair(n, both)
                 elif n < ALL_PAIRS:
                     regroup(n, nc.vector.tensor_copy, RUN, both, vector_columns)
-                if unit < UNITS - 2:
+                if unit != UNITS - 2:
                     round_state(unit, "vector", all_columns)
-                elif unit == UNITS - 1:
-                    round_state(unit, "vector", all_columns)
+                if unit == UNITS - 1:
+                    quantise_states(unit // TWIN, 1, TWIN)
                 if more_w2 and step == SET_UNITS - 2:
                     quantise_w2(q + 1)
-            if unit - LAG == UNITS - 2:
-                for k in range(TWIN):
-                    quantise_states(UNITS // TWIN - 1, k, k + 1)
             if unit >= LAG:
                 second_stage(unit - LAG)

@@ -258,16 +258,16 @@ def tile_stateencoder_pa_k_kernel(
 
         def regroup_by_tensor(n, halves, columns):
             grouped, raw = grouped_and_raw(n, halves)
-            width = columns.stop - columns.start
-            packed = bank_pool.tile([P, width, PACK], BF16, name="packed", tag="bank")
+            count, width = halves.stop - halves.start, columns.stop - columns.start
+            packed = bank_pool.tile([P, count, width, PACK], BF16, name="packed", tag="bank")
             nc.tensor.matmul(
                 out=packed[:],
                 lhsT=ident_bf[:],
-                rhs=raw[:, :, columns].rearrange("p u c -> p c u"),
+                rhs=raw[:, :, columns].rearrange("p (h u) c -> p h c u", u=PACK),
                 start=True,
                 stop=True,
             )
-            nc.scalar.copy(out=grouped[:, halves.start, columns, :], in_=packed[:])
+            nc.scalar.copy(out=grouped[:, halves, columns, :], in_=packed[:])
 
         def load_again(n):
             g, k = divmod(n, len(STREAMS))
@@ -480,15 +480,12 @@ def tile_stateencoder_pa_k_kernel(
                 i, blk = divmod(step, BLOCKS)
                 more_w2 = (q + 1) * W2_SET < GROUPS
                 scalar_work = {s: [] for s in STREAMS}
-                if n < ALL_PAIRS:
-                    half = half_i if odd else half_j
+                if n < ALL_PAIRS and not odd:
                     scalar_work["sp"].append(
-                        lambda n=n, half=half: regroup_by_tensor(n, half, tensor_columns)
+                        lambda n=n: regroup_by_tensor(n, both, tensor_columns)
                     )
                     scalar_work["sp"].append(
-                        lambda n=n, half=half: regroup(
-                            n, nc.scalar.copy, SCALAR_RUN, half, scalar_columns
-                        )
+                        lambda n=n: regroup(n, nc.scalar.copy, SCALAR_RUN, both, scalar_columns)
                     )
                 if more_w2 and blk == 1:
                     scalar_work["utt"].append(

from contextlib import ExitStack

import concourse.masks as masks
import concourse.mybir as mybir

F32 = mybir.dt.float32
BF16 = mybir.dt.bfloat16
U32 = mybir.dt.uint32
U8 = mybir.dt.uint8
I32 = mybir.dt.int32
FP8X4 = mybir.dt.float8_e4m3fn_x4
ACT = mybir.ActivationFunctionType
ALU = mybir.AluOpType

P = 128
PACK = 4
K_PASS = P * PACK
WORD = 4
RUN = 4
SCALAR_RUN = 8
B, L, D, H, OUT = 8, 16, 512, 8192, 128
TOKENS = B * L
PAIRS = B * L * L
BANK = 512
BLOCKS = PAIRS // BANK
GROUPS = H // K_PASS
UNITS = GROUPS * BLOCKS
TWIN = 2
W2_SET = 4
SET_UNITS = W2_SET * BLOCKS
STREAMS = ("sp", "utt")
SIDES = ("j", "i")
HALVES = len(SIDES)
ALL_PAIRS = GROUPS * len(STREAMS)
LAG = 5
AHEAD = 3
LEAD = 3
SCALAR_COLUMNS = 104
TENSOR_COLUMNS = 64
MAX_LOGIT_GAP = 40.0

FLOPS = 4 * 2 * TOKENS * D * H + 2 * PAIRS * H * OUT


def tile_stateencoder_pa_k_kernel(
    tc, global_outputs, sp_outputs, W_utt, b_utt, W_sp, b_sp, W2, b2, mix_w, gamma, out
):
    nc = tc.nc
    tokens_dram = {"utt": global_outputs, "sp": sp_outputs}
    weights_dram = {"utt": W_utt, "sp": W_sp}
    bias_first_column = {"utt": 0, "sp": H // P}

    with ExitStack() as ctx:
        ctx.enter_context(tc.manual_schedule())
        const = ctx.enter_context(tc.tile_pool(name="const", bufs=1))
        stage = ctx.enter_context(tc.tile_pool(name="stage", bufs=1))
        raw_pool = ctx.enter_context(tc.tile_pool(name="raw", bufs=4))
        grouped_pool = ctx.enter_context(tc.tile_pool(name="grouped", bufs=2))
        weight_pool = ctx.enter_context(tc.tile_pool(name="weights", bufs=3))
        hidden_pool = ctx.enter_context(tc.tile_pool(name="hidden", bufs=AHEAD + 1))
        state_pool = ctx.enter_context(tc.tile_pool(name="state", bufs=2))
        result_pool = ctx.enter_context(tc.tile_pool(name="result", bufs=3))
        acc_pool = ctx.enter_context(tc.psum_pool(name="acc", bufs=1))
        bank_pool = ctx.enter_context(tc.psum_pool(name="bank", bufs=4))

        warm = const.tile([P, 1], F32, name="warm")
        nc.vector.memset(warm[:], 0.0)
        warm_out = const.tile([P, 1], F32, name="warm_out")
        nc.scalar.activation(out=warm_out[:], in_=warm[:], func=ACT.Exp)

        b2_rows = const.tile([P, P], BF16, name="b2_rows")
        nc.gpsimd.memset(b2_rows[:], 0.0)
        ident_bf = const.tile([P, P], BF16, name="ident_bf")
        masks.make_identity(nc, ident_bf[:])

        raw_groups = {}

        def load_weights(g, s, pieces):
            hidden_range = slice(g * K_PASS, (g + 1) * K_PASS)
            raw = raw_pool.tile([P, HALVES * PACK, K_PASS], BF16, name="raw_" + s, tag="raw_w")
            rows = weights_dram[s][:, hidden_range].rearrange("(v q) w -> q v w", q=P)
            step = HALVES * PACK // pieces
            for v in range(0, HALVES * PACK, step):
                nc.sync.dma_start(out=raw[:, v : v + step, :], in_=rows[:, v : v + step, :])
            raw_groups[g, s] = raw

        def load_w2(q):
            raw = raw_pool.tile([P, W2_SET * PACK, OUT], BF16, name="raw_w2", bufs=2)
            w2_rows = W2_SET * K_PASS
            nc.sync.dma_start(
                out=raw[:],
                in_=W2[q * w2_rows : (q + 1) * w2_rows, :].rearrange("(v p) o -> p v o", p=P),
            )
            raw_groups[q, "W2"] = raw

        token_rows = {}

        def load_tokens(s):
            token_rows[s] = const.tile([P, D], BF16, name="token_rows_" + s)
            nc.sync.dma_start(
                out=token_rows[s][:], in_=tokens_dram[s].rearrange("b l d -> (b l) d")
            )

        for s in STREAMS:
            load_tokens(s)
            load_weights(0, s, HALVES)

        bias_rows = const.tile([P, P], BF16, name="bias_rows")
        nc.sync.dma_start(out=bias_rows[0 : H // P, :], in_=b_utt.rearrange("(c p) -> c p", p=P))
        nc.sync.dma_start(out=bias_rows[H // P : P, :], in_=b_sp.rearrange("(c p) -> c p", p=P))
        nc.sync.dma_start(out=b2_rows[0:1, :], in_=b2.rearrange("(r c) -> r c", r=1))
        mix_bf = const.tile([P, 2], BF16, name="mix_bf")
        nc.sync.dma_start(out=mix_bf[:], in_=mix_w.partition_broadcast(P))
        gamma_bf = const.tile([P, 1], BF16, name="gamma_bf")
        nc.sync.dma_start(out=gamma_bf[:], in_=gamma.partition_broadcast(P))
        load_w2(0)
        for s in STREAMS:
            load_weights(1, s, 1)


        token_grouped = {}

        def turn_tokens(s):
            flipped = bank_pool.tile([P, PACK, TOKENS], BF16, name="flipped", tag="bank")
            for u in range(PACK):
                nc.tensor.transpose(
                    flipped[:, u, :], token_rows[s][:, u * P : (u + 1) * P], ident_bf[:]
                )
            token_grouped[s] = const.tile(
                [P, TOKENS, PACK], BF16, name="token_grouped_" + s, align_bytes=64
            )
            copy = nc.vector.tensor_copy if s == STREAMS[0] else nc.scalar.copy
            copy(out=token_grouped[s][:], in_=flipped[:].rearrange("p u r -> p r u"))

        bias_cols = const.tile([P, P], F32, name="bias_cols")
        b2_col = const.tile([P, 1], F32, name="b2_col")

        def turn_biases():
            bias_flipped = bank_pool.tile([P, P], BF16, name="bias_flipped", tag="bank")
            nc.tensor.transpose(bias_flipped[:], bias_rows[:], ident_bf[:])
            nc.scalar.copy(out=bias_cols[:], in_=bias_flipped[:])
            b2_flipped = bank_pool.tile([P, P], BF16, name="b2_flipped", tag="bank")
            nc.tensor.transpose(b2_flipped[:], b2_rows[:], ident_bf[:])
            nc.scalar.copy(out=b2_col[:], in_=b2_flipped[:, 0:1])

        pair_codes = {}
        pair_scales = {}
        token_planes = {}
        for s in STREAMS:
            for side, columns in (("i", BANK), ("j", PAIRS)):
                pair_codes[s, side] = const.tile(
                    [P, columns], U32, name="pair_codes_%s_%s" % (s, side), align_bytes=64
                )
                pair_scales[s, side] = const.tile(
                    [P, columns], U8, name="pair_scales_%s_%s" % (s, side), align_bytes=64
                )
            token_codes = const.tile([P, TOKENS], U32, name="token_codes_" + s, align_bytes=64)
            token_scales = const.tile([P, TOKENS], U8, name="token_scales_" + s, align_bytes=64)
            nc.gpsimd.memset(token_scales[:].bitcast(I32), 0)
            token_planes[s] = (token_codes, token_scales)

        ident_f32 = const.tile([P, P], F32, name="ident_f32")
        masks.make_identity(nc, ident_f32[:])

        def quantise_tokens(s):
            grouped = token_grouped[s]
            token_codes, token_scales = token_planes[s]
            fourfold = stage.tile([P, TOKENS, WORD, PACK], BF16, name="fourfold", align_bytes=64)
            nc.vector.tensor_copy(
                out=fourfold[:], in_=grouped[:].unsqueeze(2).to_broadcast([P, TOKENS, WORD, PACK])
            )
            nc.vector.quantize_mx(
                out=token_codes[:].bitcast(FP8X4),
                scales=token_scales[:],
                in_=grouped[:].rearrange("p r u -> p (r u)"),
            )
            nc.vector.quantize_mx(
                out=pair_codes[s, "i"][:].bitcast(FP8X4),
                scales=pair_scales[s, "i"][:],
                in_=fourfold[:].rearrange("p r f u -> p (r f u)"),
            )

        def repeat_side_j(s, first, last):
            token_codes, token_scales = token_planes[s]
            columns = slice(first * BANK, last * BANK)
            blocks = last - first
            nc.vector.tensor_copy(
                out=pair_codes[s, "j"][:, columns]
                .bitcast(I32)
                .rearrange("p (k b i j) -> p b k i j", k=blocks, b=B, j=WORD),
                in_=token_codes[:]
                .bitcast(I32)
                .rearrange("p (b k j) -> p b k j", b=B, j=WORD)[:, :, first:last, :]
                .unsqueeze(3)
                .to_broadcast([P, B, blocks, L, WORD]),
            )
            nc.vector.tensor_copy(
                out=pair_scales[s, "j"][:, columns]
                .bitcast(I32)
                .rearrange("p (k b i) -> p b k i", k=blocks, b=B),
                in_=token_scales[:]
                .bitcast(I32)
                .rearrange("p (b k) -> p b k", b=B)[:, :, first:last]
                .unsqueeze(3)
                .to_broadcast([P, B, blocks, L]),
            )

        mix = const.tile([P, 2], F32, name="mix")
        gain = const.tile([P, 1], F32, name="gain")
        gap = const.tile([P, 1], F32, name="gap")
        ratio = const.tile([P, 1], F32, name="ratio")
        denominator = const.tile([P, 1], F32, name="denominator")
        weight_sp = const.tile([P, 1], F32, name="weight_sp")
        gain_sp = const.tile([P, 1], F32, name="gain_sp")

        def mix_weights():
            nc.gpsimd.tensor_copy(out=mix[:], in_=mix_bf[:])
            nc.gpsimd.tensor_copy(out=gain[:], in_=gamma_bf[:])
            nc.gpsimd.tensor_scalar(
                out=gap[:],
                in0=mix[:, 0:1],
                scalar1=mix[:, 1:2],
                scalar2=MAX_LOGIT_GAP,
                op0=ALU.subtract,
                op1=ALU.min,
            )
            nc.scalar.activation(out=ratio[:], in_=gap[:], func=ACT.Exp)
            nc.gpsimd.tensor_scalar_add(out=denominator[:], in0=ratio[:], scalar1=1.0)
            nc.vector.reciprocal(out=weight_sp[:], in_=denominator[:])
            nc.gpsimd.tensor_mul(out=gain_sp[:], in0=weight_sp[:], in1=gain[:])

        half_j, half_i, both = slice(0, 1), slice(1, 2), slice(0, HALVES)
        all_columns = slice(0, K_PASS)
        vector_columns = slice(0, K_PASS - SCALAR_COLUMNS - TENSOR_COLUMNS)
        tensor_columns = slice(vector_columns.stop, vector_columns.stop + TENSOR_COLUMNS)
        scalar_columns = slice(K_PASS - SCALAR_COLUMNS, K_PASS)
        grouped_pairs = {}
        grouped_w2 = {}
        weight_operands = {}

        def grouped_and_raw(n, halves):
            g, k = divmod(n, len(STREAMS))
            if n not in grouped_pairs:
                grouped_pairs[n] = grouped_pool.tile(
                    [P, HALVES, K_PASS, PACK], BF16, name="grouped", align_bytes=64
                )
            rows = slice(halves.start * PACK, halves.stop * PACK)
            return grouped_pairs[n], raw_groups[g, STREAMS[k]][:, rows, :]

        def regroup(n, copy, run, halves, columns):
            grouped, raw = grouped_and_raw(n, halves)
            copy(
                out=grouped[:, halves, columns, :].rearrange(
                    "p h (c i) u -> p h c u i", i=run
                ),
                in_=raw[:, :, columns].rearrange("p (h u) (c i) -> p h c u i", u=PACK, i=run),
            )

        def regroup_by_tensor(n, halves, columns):
            grouped, raw = grouped_and_raw(n, halves)
            count, width = halves.stop - halves.start, columns.stop - columns.start
            packed = bank_pool.tile([P, count, width, PACK], BF16, name="packed", tag="bank")
            nc.tensor.matmul(
                out=packed[:],
                lhsT=ident_bf[:],
                rhs=raw[:, :, columns].rearrange("p (h u) c -> p h c u", u=PACK),
                start=True,
                stop=True,
            )
            nc.scalar.copy(out=grouped[:, halves, columns, :], in_=packed[:])

        def load_again(n):
            g, k = divmod(n, len(STREAMS))
            if g + 2 < GROUPS:
                load_weights(g + 2, STREAMS[k], 1)

        def quantise_pair(n, halves):
            g, k = divmod(n, len(STREAMS))
            s = STREAMS[k]
            if halves.start == 0:
                weight_operands[g, s] = (
                    weight_pool.tile([P, HALVES, K_PASS], U32, name="w_codes_" + s, align_bytes=64),
                    weight_pool.tile([P, HALVES, K_PASS], U8, name="w_scales_" + s, align_bytes=64),
                )
            w_codes, w_scales = weight_operands[g, s]
            nc.vector.quantize_mx(
                out=w_codes[:, halves, :].rearrange("p h w -> p (h w)").bitcast(FP8X4),
                scales=w_scales[:, halves, :].rearrange("p h w -> p (h w)"),
                in_=grouped_pairs[n][:, halves, :, :].rearrange("p h w u -> p (h w u)"),
            )

        def regroup_w2(q, copy, run, first, last):
            if first == 0:
                grouped_w2[q] = grouped_pool.tile(
                    [P, W2_SET, OUT, PACK], BF16, name="grouped_w2", bufs=1, align_bytes=64
                )
            copy(
                out=grouped_w2[q][:, first:last, :, :].rearrange("p g (c i) t -> p g c t i", i=run),
                in_=raw_groups[q, "W2"][:, first * PACK : last * PACK, :].rearrange(
                    "p (g t) (c i) -> p g c t i", t=PACK, i=run
                ),
            )
            if last == W2_SET and (q + 1) * W2_SET < GROUPS:
                load_w2(q + 1)

        def quantise_w2(q):
            w2_codes = weight_pool.tile([P, W2_SET, OUT], U32, name="w2_codes", bufs=2, align_bytes=64)
            w2_scales = weight_pool.tile([P, W2_SET, OUT], U8, name="w2_scales", bufs=2, align_bytes=64)
            nc.vector.quantize_mx(
                out=w2_codes[:].rearrange("p g o -> p (g o)").bitcast(FP8X4),
                scales=w2_scales[:].rearrange("p g o -> p (g o)"),
                in_=grouped_w2[q][:].rearrange("p g o t -> p (g o t)"),
            )
            for i in range(W2_SET):
                weight_operands[q * W2_SET + i, "W2"] = (w2_codes[:, i, :], w2_scales[:, i, :])

        acc = [acc_pool.tile([P, BANK], F32, name="acc%d" % blk) for blk in range(BLOCKS)]
        hidden_tiles = {}
        state_tiles = {}
        state_words = {}

        def first_stage(unit, scalar_work):
            g, blk = divmod(unit, BLOCKS)
            side_range = {"i": slice(0, BANK), "j": slice(blk * BANK, (blk + 1) * BANK)}
            for s in STREAMS:
                w_codes, w_scales = weight_operands[g, s]
                hidden = hidden_pool.tile([P, PACK, BANK], F32, name="hidden_" + s)
                for t in range(PACK):
                    chunk = slice(t * P, (t + 1) * P)
                    bank = bank_pool.tile([P, BANK], F32, name="bank", tag="bank")
                    for half, side in enumerate(SIDES):
                        nc.tensor.matmul_mx(
                            out=bank[:],
                            lhsT=w_codes[:, half, chunk].bitcast(FP8X4),
                            lhsT_scale=w_scales[:, half, chunk],
                            rhs=pair_codes[s, side][:, side_range[side]].bitcast(FP8X4),
                            rhs_scale=pair_scales[s, side][:, side_range[side]],
                            start=(half == 0),
                            stop=(half == HALVES - 1),
                        )
                    column = bias_first_column[s] + g * PACK + t
                    nc.scalar.activation(
                        out=hidden[:, t, :],
                        in_=bank[:],
                        func=ACT.Tanh,
                        bias=bias_cols[:, column : column + 1],
                        scale=1.0,
                    )
                hidden_tiles[unit, s] = hidden
                for work in scalar_work[s]:
                    work()

        def mix_streams(unit, chunks):
            hidden_utt = hidden_tiles[unit, "utt"]
            nc.vector.scalar_tensor_tensor(
                out=hidden_utt[:, chunks, :],
                in0=hidden_utt[:, chunks, :],
                scalar=ratio[:, 0:1],
                in1=hidden_tiles[unit, "sp"][:, chunks, :],
                op0=ALU.mult,
                op1=ALU.add,
            )

        def round_state(unit, engine, columns):
            twin, k = divmod(unit, TWIN)
            if twin not in state_tiles:
                state_tiles[twin] = state_pool.tile(
                    [P, TWIN, BANK, PACK], BF16, name="state", align_bytes=64
                )
            packed = state_tiles[twin][:, k, columns, :].rearrange("p (c i) t -> p c t i", i=RUN)
            mixed = hidden_tiles[unit, "utt"][:, :, columns].rearrange(
                "p t (c i) -> p c t i", i=RUN
            )
            if engine == "vector":
                nc.vector.tensor_scalar(
                    out=packed, in0=mixed, scalar1=gain_sp[:, 0:1], scalar2=None, op0=ALU.mult
                )
            else:
                nc.scalar.activation(out=packed, in_=mixed, func=ACT.Copy, scale=gain_sp[:, 0:1])

        def quantise_states(twin, first, last):
            if first == 0:
                state_words[twin] = (
                    state_pool.tile([P, TWIN, BANK], U32, name="state_codes", bufs=3, align_bytes=64),
                    state_pool.tile([P, TWIN, BANK], U8, name="state_scales", bufs=3, align_bytes=64),
                )
            state_codes, state_scales = state_words[twin]
            nc.vector.quantize_mx(
                out=state_codes[:, first:last, :].rearrange("p k c -> p (k c)").bitcast(FP8X4),
                scales=state_scales[:, first:last, :].rearrange("p k c -> p (k c)"),
                in_=state_tiles[twin][:, first:last, :, :].rearrange("p k c t -> p (k c t)"),
            )

        out_rows = out.rearrange("b i (k j) o -> k (b i) j o", j=WORD)

        results = {}

        def parts(blk):
            step = WORD // 2 if blk == BLOCKS - 1 else WORD
            return [slice(first, first + step) for first in range(0, WORD, step)]

        def squash_block(blk):
            columns = acc[blk][:].rearrange("p (r j) -> p j r", j=WORD)
            for part in parts(blk):
                result = result_pool.tile([P, part.stop - part.start, TOKENS], F32, name="result")
                nc.scalar.activation(
                    out=result[:],
                    in_=columns[:, part, :],
                    func=ACT.Tanh,
                    bias=b2_col[:, 0:1],
                    scale=1.0,
                )
                results[blk, part.start] = result

        def store_block(blk):
            for part in parts(blk):
                result = results[blk, part.start]
                turned = bank_pool.tile(
                    [P, part.stop - part.start, OUT], F32, name="turned", tag="bank"
                )
                for j in range(part.stop - part.start):
                    nc.tensor.transpose(turned[:, j, :], result[:, j, :], ident_f32[:])
                result_rows = result_pool.tile(
                    [P, part.stop - part.start, OUT], F32, name="result_rows"
                )
                copy = nc.vector.tensor_copy if part.stop < WORD else nc.scalar.copy
                copy(out=result_rows[:], in_=turned[:])
                nc.sync.dma_start(out=out_rows[blk][:, part, :], in_=result_rows[:])

        def second_stage(unit):
            g, blk = divmod(unit, BLOCKS)
            w2_codes, w2_scales = weight_operands[g, "W2"]
            twin, k = divmod(unit, TWIN)
            state_codes, state_scales = state_words[twin]
            nc.tensor.matmul_mx(
                out=acc[blk][:],
                lhsT=w2_codes.bitcast(FP8X4),
                lhsT_scale=w2_scales,
                rhs=state_codes[:, k, :].bitcast(FP8X4),
                rhs_scale=state_scales[:, k, :],
                start=(g == 0),
                stop=(g == GROUPS - 1),
            )
            if g == GROUPS - 1:
                squash_block(blk)
                if blk > 0:
                    for ready in (0, 1) if blk == 1 else (blk,):
                        store_block(ready)

        turn_tokens("sp")
        regroup(0, nc.scalar.copy, SCALAR_RUN, half_j, all_columns)
        turn_tokens("utt")
        quantise_tokens("sp")
        repeat_side_j("sp", 0, 1)
        quantise_pair(0, half_j)
        regroup(0, nc.vector.tensor_copy, RUN, half_i, all_columns)
        load_again(0)
        turn_biases()
        regroup(1, nc.scalar.copy, SCALAR_RUN, half_j, all_columns)
        quantise_pair(0, half_i)
        quantise_tokens("utt")
        repeat_side_j("utt", 0, 1)
        regroup(1, nc.vector.tensor_copy, RUN, half_i, all_columns)
        load_again(1)
        mix_weights()
        quantise_pair(1, both)
        for s in STREAMS:
            repeat_side_j(s, 1, BLOCKS)
        regroup_w2(0, nc.vector.tensor_copy, RUN, 0, W2_SET)
        regroup(2, nc.vector.tensor_copy, RUN, both, all_columns)
        load_again(2)
        quantise_w2(0)
        quantise_pair(2, both)

        for unit in range(UNITS + LAG):
            if unit < UNITS:
                n, odd = divmod(unit, TWIN)
                n += LEAD
                q, step = divmod(unit, SET_UNITS)
                i, blk = divmod(step, BLOCKS)
                more_w2 = (q + 1) * W2_SET < GROUPS
                scalar_work = {s: [] for s in STREAMS}
                if n < ALL_PAIRS and not odd:
                    scalar_work["sp"].append(
                        lambda n=n: regroup_by_tensor(n, both, tensor_columns)
                    )
                    scalar_work["sp"].append(
                        lambda n=n: regroup(n, nc.scalar.copy, SCALAR_RUN, both, scalar_columns)
                    )
                if more_w2 and blk == 1:
                    scalar_work["utt"].append(
                        lambda q=q, i=i: regroup_w2(q + 1, nc.scalar.copy, SCALAR_RUN, i, i + 1)
                    )
                first_stage(unit, scalar_work)
                if unit < UNITS - 1:
                    mix_streams(unit, slice(0, PACK))
                else:
                    round_state(unit - 1, "scalar", all_columns)
                    for chunk in range(PACK):
                        if chunk == PACK // 2:
                            quantise_states(unit // TWIN, 0, 1)
                        mix_streams(unit, slice(chunk, chunk + 1))
                if unit > 0 and not odd:
                    quantise_states(unit // TWIN - 1, 0, TWIN)
                if n < ALL_PAIRS and odd:
                    load_again(n)
                    quantise_pair(n, both)
                elif n < ALL_PAIRS:
                    regroup(n, nc.vector.tensor_copy, RUN, both, vector_columns)
                if unit != UNITS - 2:
                    round_state(unit, "vector", all_columns)
                if unit == UNITS - 1:
                    quantise_states(unit // TWIN, 1, TWIN)
                if more_w2 and step == SET_UNITS - 2:
                    quantise_w2(q + 1)
            if unit >= LAG:
                second_stage(unit - LAG)
